import numpy as np
import ml_dtypes


def mxq(x, axis, fmt="e4m3"):
    dtype, down = {"e4m3": (ml_dtypes.float8_e4m3fn, 7), "e5m2": (ml_dtypes.float8_e5m2, 14)}[fmt]
    v = np.moveaxis(np.asarray(x, np.float32).astype(ml_dtypes.bfloat16).astype(np.float64), axis, -1)
    blocks = v.reshape(v.shape[:-1] + (-1, 32))
    amax = np.abs(blocks).max(-1, keepdims=True)
    byte = np.maximum(np.where(amax > 0, np.frexp(amax)[1] - 1 + 127, 0) - down, 1)
    scale = np.exp2(byte - 127.0)
    codes = (blocks / scale).astype(np.float32).astype(dtype).astype(np.float64)
    return np.moveaxis((codes * scale).reshape(v.shape), -1, axis)


WIDE = False


def mx_kscale(k):
    if not WIDE:
        return np.ones(k)
    levels = np.array([10, -10, 5, -5, 0])
    a = np.random.permutation(np.resize(levels, k // 512 * 4)).reshape(k // 512, 4)
    idx = np.arange(k)
    return np.exp2(a[idx // 512, idx % 128 // 32])


BF16 = ml_dtypes.bfloat16


def bf(x):
    return np.asarray(x, np.float32).astype(BF16)


def f64(x):
    return np.asarray(x).astype(np.float64)


B, NT, N, C, DV, TM = 2, 128, 512, 1024, 1024, 128
LN_EPS = 1e-5


def layernorm(h, gamma, beta):
    mu = h.mean(-1, keepdims=True)
    var = np.square(h - mu).mean(-1, keepdims=True)
    return (h - mu) / np.sqrt(var + LN_EPS) * gamma + beta


def setup_inputs():
    t = mx_kscale(DV)
    return {'q': bf(np.random.standard_normal((B, NT, C)) * 1.4),
            'k': bf(np.random.standard_normal((B, N, C)) * 1.4),
            'ki': bf(np.random.standard_normal((B, N, C)) * 1.4),
            'v': bf(np.random.standard_normal((B, N, DV)) * 1.8 * t),
            'vi': bf(np.random.standard_normal((B, N, DV)) * 1.8 * t),
            'T': bf(np.random.standard_normal((B, NT, C))),
            'Wout': bf(np.random.standard_normal((DV, C)) * 1.5 / np.sqrt(DV) / t[:, None]),
            'gamma': bf(1.0 + 0.1 * np.random.standard_normal(C)),
            'beta': bf(0.1 * np.random.standard_normal(C))}


def reference(q, k, ki, v, vi, T, Wout, gamma, beta):
    scale = C ** -0.5
    wo = mxq(f64(Wout), 0, 'e4m3')
    s = f64(q) @ f64(k).transpose(0, 2, 1) * scale
    e = np.exp(s - s.max(-1, keepdims=True))
    o = (mxq(e, 2, 'e4m3') @ mxq(f64(v), 1, 'e4m3')) / e.sum(-1, keepdims=True)
    x_out = mxq(o, 2, 'e4m3') @ wo
    si = f64(q) @ f64(ki).transpose(0, 2, 1) * scale
    ei = np.exp(si - si.max(-1, keepdims=True))
    oi = (mxq(ei, 2, 'e4m3') @ mxq(f64(vi), 1, 'e4m3')) / ei.sum(-1, keepdims=True)
    xi_out = mxq(oi, 2, 'e4m3') @ wo
    return layernorm(f64(T) + x_out + xi_out, f64(gamma), f64(beta))

@@ -1,0 +1,406 @@
+from contextlib import ExitStack
+
+import concourse.mybir as mybir
+from concourse.masks import make_identity
+
+F32 = mybir.dt.float32
+BF16 = mybir.dt.bfloat16
+I32 = mybir.dt.int32
+U32 = mybir.dt.uint32
+U8 = mybir.dt.uint8
+FP8X4 = mybir.dt.float8_e4m3fn_x4
+ACT = mybir.ActivationFunctionType
+ALU = mybir.AluOpType
+AX = mybir.AxisListType
+
+P = 128
+B = 2
+NK = 512
+C = 1024
+DV = 1024
+HALF = 512
+SCALE = 1.0 / 32.0
+EPS = 1e-5
+FLOPS = 4 * (2 * P * NK * C + 2 * P * NK * DV + 2 * P * DV * C)
+W_CHUNKS_AFTER_UNIT = [1,2,1,0]
+
+
+def tile_crossattention_for_fusion_temporal_pb_kernel(tc, q, k, ki, v, vi, T, Wout, gamma, beta, out):
+    nc = tc.nc
+    with ExitStack() as ctx:
+        const = ctx.enter_context(tc.tile_pool(name="const", bufs=1))
+        raw = ctx.enter_context(tc.tile_pool(name="raw", bufs=1))
+        keep = ctx.enter_context(tc.tile_pool(name="keep", bufs=1))
+        small = ctx.enter_context(tc.tile_pool(name="small", bufs=1))
+        work = ctx.enter_context(tc.tile_pool(name="work", bufs=2))
+        psum = ctx.enter_context(tc.psum_pool(name="psum", bufs=8))
+        ctx.enter_context(tc.manual_schedule())
+
+        units = [(b, s) for b in range(B) for s in range(2)]
+        key_src = (k, ki)
+        val_src = (v, vi)
+
+        def half(n):
+            return slice(HALF * n, HALF * (n + 1))
+
+        gb_row = const.tile([P, 2 * C], BF16, name="gb_row")
+        nc.vector.memset(gb_row[:].bitcast(I32), 0)
+        ones_b = const.tile([P, P], BF16, name="ones_b")
+        nc.vector.memset(ones_b[:], 1.0)
+        ident_f = const.tile([P, P], F32, name="ident_f")
+        make_identity(nc, ident_f[:])
+        ident_b = const.tile([P, P], BF16, name="ident_b")
+        make_identity(nc, ident_b[:])
+        mhalf = const.tile([P, 1], F32, name="mhalf")
+        nc.gpsimd.memset(mhalf[:], -0.5)
+
+        q_sb = [raw.tile([P, C], BF16, name="q_sb%d" % b) for b in range(B)]
+        k_sb = [raw.tile([P, 4, C], BF16, name="k_sb%d" % i) for i in range(4)]
+        v_sb = [raw.tile([P, 4, DV], BF16, name="v_sb%d" % i) for i in range(4)]
+        w_sb = raw.tile([P, 2, 4, C], BF16, name="w_sb")
+        t_sb = raw.tile([P, B, C], BF16, name="t_sb")
+
+        def load_gamma_beta():
+            nc.sync.dma_start(out=gb_row[0:1, 0:C], in_=gamma.rearrange("(o c) -> o c", o=1))
+            nc.sync.dma_start(out=gb_row[0:1, C : 2 * C], in_=beta.rearrange("(o c) -> o c", o=1))
+
+        def load_q(b):
+            nc.sync.dma_start(out=q_sb[b][:], in_=q[b, :, :])
+
+        def load_k(i):
+            b, s = units[i]
+            nc.sync.dma_start(out=k_sb[i][:], in_=key_src[s][b, :, :].rearrange("(p a) c -> p a c", a=4))
+
+        def load_v(i):
+            b, s = units[i]
+            nc.sync.dma_start(out=v_sb[i][:], in_=val_src[s][b, :, :].rearrange("(p j) w -> p j w", j=4))
+
+        def load_w(g):
+            nc.sync.dma_start(out=w_sb[:, g, :, :], in_=Wout.rearrange("(g t p) n -> g p t n", g=2, t=4, p=P)[g])
+
+        def load_t():
+            nc.sync.dma_start(out=t_sb[:], in_=T.rearrange("b p c -> p b c"))
+
+        load_gamma_beta()
+        load_q(0)
+        load_k(0)
+        load_v(0)
+        load_k(1)
+        load_v(1)
+        load_w(0)
+        load_q(1)
+        load_k(2)
+        load_v(2)
+        load_w(1)
+        load_t()
+        load_k(3)
+        load_v(3)
+
+        gb_bc = const.tile([P, 2, C], BF16, name="gb_bc")
+        for i in range(2):
+            gp = psum.tile([P, C], BF16, tag="bank", name="gp%d" % i)
+            for n in range(2):
+                nc.tensor.matmul(
+                    out=gp[:, half(n)],
+                    lhsT=ones_b[:],
+                    rhs=gb_row[:, C * i + HALF * n : C * i + HALF * (n + 1)],
+                    start=True,
+                    stop=True,
+                )
+            nc.vector.tensor_copy(out=gb_bc[:, i, :], in_=gp[:])
+
+        qT = [keep.tile([P, 4, P], F32, name="qT%d" % b) for b in range(B)]
+        kT = {}
+        sc = {}
+        nb = {}
+        e_sb = {}
+        rs = {}
+        rc = {}
+        eg = {}
+        vg = {}
+        ot = {}
+        og = {}
+        acc = {}
+
+        def q_transpose(b):
+            tp = psum.tile([P, 4, P], F32, tag="bank", name="qtp%d" % b)
+            words = q_sb[b][:].bitcast(F32)
+            for u in range(4):
+                nc.tensor.transpose(out=tp[:, u, :], in_=words[:, P * u : P * (u + 1)], identity=ident_f[:])
+            nc.scalar.copy(out=qT[b][:], in_=tp[:])
+
+        def k_transpose(i, vector_chunks):
+            kT[i] = work.tile([P, 4, NK], F32, tag="kT", name="kT%d" % i)
+            banks = []
+            for u in range(4):
+                tp = psum.tile([P, 4, P], F32, tag="bank", name="ktp%d_%d" % (i, u))
+                for a in range(4):
+                    nc.tensor.transpose(
+                        out=tp[:, a, :],
+                        in_=k_sb[i][:, a, :].bitcast(F32)[:, P * u : P * (u + 1)],
+                        identity=ident_f[:],
+                    )
+                banks.append(tp)
+            for u in range(4):
+                copy = nc.vector.tensor_copy if u >= 4 - vector_chunks else nc.scalar.copy
+                copy(out=kT[i][:, u, :], in_=banks[u][:].rearrange("p a n -> p (a n)"))
+
+        def scores(i):
+            b = units[i][0]
+            sc[i] = psum.tile([P, NK], F32, tag="bank", name="sc%d" % i)
+            for u in range(4):
+                q_pairs = qT[b][:, u, :].bitcast(BF16).rearrange("p (m e) -> p e m", e=2)
+                k_pairs = kT[i][:, u, :].bitcast(BF16).rearrange("p (n e) -> p e n", e=2)
+                for e in range(2):
+                    nc.tensor.matmul(
+                        out=sc[i][:],
+                        lhsT=q_pairs[:, e, :],
+                        rhs=k_pairs[:, e, :],
+                        start=(u == 0 and e == 0),
+                        stop=(u == 3 and e == 1),
+                    )
+
+        def row_max(i):
+            mx = small.tile([P, 1], F32, name="mx%d" % i)
+            nc.vector.reduce_max(out=mx[:], in_=sc[i][:], axis=AX.X)
+            nb[i] = small.tile([P, 1], F32, name="nb%d" % i)
+            nc.vector.tensor_scalar(out=nb[i][:], in0=mx[:], scalar1=-SCALE, scalar2=None, op0=ALU.mult)
+
+        def exponentials(i):
+            e_sb[i] = work.tile([P, NK], BF16, tag="e_sb", name="e_sb%d" % i)
+            rs[i] = small.tile([P, 1], F32, name="rs%d" % i)
+            nc.scalar.activation(
+                out=e_sb[i][:], in_=sc[i][:], func=ACT.Exp, bias=nb[i][:], scale=SCALE, accum_out=rs[i][:]
+            )
+
+        def e_transpose(i):
+            et = psum.tile([P, 4, P], BF16, tag="bank", name="et%d" % i)
+            for a in range(4):
+                nc.tensor.transpose(out=et[:, a, :], in_=e_sb[i][:, P * a : P * (a + 1)], identity=ident_b[:])
+            eg[i] = work.tile([P, P, 4], BF16, tag="eg", name="eg%d" % i, align_bytes=64)
+            nc.scalar.copy(out=eg[i][:], in_=et[:].rearrange("p a m -> p m a"))
+
+        rt_sb = [keep.tile([P, P], F32, name="rt_sb%d" % i) for i in range(4)]
+
+        def row_sum_reciprocal(i):
+            rc[i] = small.tile([P, 1], F32, name="rc%d" % i)
+            nc.vector.reciprocal(out=rc[i][:], in_=rs[i][:])
+            rtp = psum.tile([P, P], F32, tag="bank", name="rtp%d" % i)
+            nc.tensor.matmul(
+                out=rtp[:], lhsT=rc[i][:, 0:1].to_broadcast([P, P]), rhs=ident_f[:], start=True, stop=True
+            )
+            nc.scalar.copy(out=rt_sb[i][:], in_=rtp[:])
+
+        e_codes = [keep.tile([P, P], U32, name="e_codes%d" % i, align_bytes=64) for i in range(4)]
+        e_scales = [keep.tile([P, P], U8, name="e_scales%d" % i, align_bytes=64) for i in range(4)]
+
+        def e_quantise(i):
+            nc.vector.quantize_mx(
+                out=e_codes[i][:].bitcast(FP8X4),
+                scales=e_scales[i][:],
+                in_=eg[i][:].rearrange("p m a -> p (m a)"),
+            )
+
+        def regroup(copy, dst, src):
+            copy(
+                out=dst.rearrange("p (c i) t -> p c t i", i=4),
+                in_=src.rearrange("p t (c i) -> p c t i", i=4),
+            )
+
+        v_codes = [keep.tile([P, DV], U32, name="v_codes%d" % i, align_bytes=64) for i in range(4)]
+        v_scales = [keep.tile([P, DV], U8, name="v_scales%d" % i, align_bytes=64) for i in range(4)]
+
+        def v_regroup(i, h):
+            if h == 0:
+                vg[i] = work.tile([P, DV, 4], BF16, tag="vg", name="vg%d" % i, align_bytes=64)
+            regroup(nc.vector.tensor_copy, vg[i][:, half(h), :], v_sb[i][:, :, half(h)])
+
+        def v_quantise(i, h):
+            nc.vector.quantize_mx(
+                out=v_codes[i][:, half(h)].bitcast(FP8X4),
+                scales=v_scales[i][:, half(h)],
+                in_=vg[i][:, half(h), :].rearrange("p w j -> p (w j)"),
+            )
+
+        o_codes = [keep.tile([P, 2 * P], U32, name="o_codes%d" % i, align_bytes=64) for i in range(4)]
+        o_scales = [keep.tile([P, 2 * P], U8, name="o_scales%d" % i, align_bytes=64) for i in range(4)]
+
+        def attend(i):
+            for g in range(2):
+                ot[i, g] = psum.tile([P, 4, P], F32, tag="bank", name="ot%d_%d" % (i, g))
+                for t in range(4):
+                    cols = slice(P * (4 * g + t), P * (4 * g + t + 1))
+                    nc.tensor.matmul_mx(
+                        out=ot[i, g][:, t, :],
+                        lhsT=v_codes[i][:, cols].bitcast(FP8X4),
+                        lhsT_scale=v_scales[i][:, cols],
+                        rhs=e_codes[i][:].bitcast(FP8X4),
+                        rhs_scale=e_scales[i][:],
+                        start=True,
+                        stop=True,
+                    )
+
+        def o_divide(i, g):
+            if g == 0:
+                og[i] = work.tile([P, 2, P, 4], BF16, tag="og", name="og%d" % i, align_bytes=64)
+            nc.vector.tensor_tensor(
+                out=og[i][:, g, :, :],
+                in0=ot[i, g][:].rearrange("p t m -> p m t"),
+                in1=rt_sb[i][:].unsqueeze(2).to_broadcast([P, P, 4]),
+                op=ALU.mult,
+            )
+
+        def o_quantise(i, g0, g1):
+            cols = slice(P * g0, P * g1)
+            nc.vector.quantize_mx(
+                out=o_codes[i][:, cols].bitcast(FP8X4),
+                scales=o_scales[i][:, cols],
+                in_=og[i][:, g0:g1, :, :].rearrange("p g m t -> p (g m t)"),
+            )
+
+        w_codes = keep.tile([P, 2, C], U32, name="w_codes", align_bytes=64)
+        w_scales = keep.tile([P, 2, C], U8, name="w_scales", align_bytes=64)
+        wg = keep.tile([P, 2, C, 4], BF16, name="wg", align_bytes=64)
+
+        def w_regroup(j):
+            g, n = divmod(j, 2)
+            regroup(nc.scalar.copy, wg[:, g, half(n), :], w_sb[:, g, :, half(n)])
+
+        def w_quantise(j):
+            g, n = divmod(j, 2)
+            nc.vector.quantize_mx(
+                out=w_codes[:, g, half(n)].bitcast(FP8X4),
+                scales=w_scales[:, g, half(n)],
+                in_=wg[:, g, half(n), :].rearrange("p w j -> p (w j)"),
+            )
+
+        def project(b, s):
+            i = 2 * b + s
+            for g in range(2):
+                rows = slice(P * g, P * (g + 1))
+                for n in range(2):
+                    if s == 0 and g == 0:
+                        acc[b, n] = psum.tile([P, HALF], F32, tag="bank", name="acc%d_%d" % (b, n))
+                    nc.tensor.matmul_mx(
+                        out=acc[b, n][:],
+                        lhsT=o_codes[i][:, rows].bitcast(FP8X4),
+                        lhsT_scale=o_scales[i][:, rows],
+                        rhs=w_codes[:, g, half(n)].bitcast(FP8X4),
+                        rhs_scale=w_scales[:, g, half(n)],
+                        start=(s == 0 and g == 0),
+                        stop=(s == 1 and g == 1),
+                    )
+
+        h = {}
+        negmu = {}
+        t1 = {}
+        rstd = {}
+
+        def residual_and_mean(b):
+            h[b] = work.tile([P, C], F32, tag="h", name="h%d" % b)
+            hs = small.tile([P, 2], F32, name="hs%d" % b)
+            for n in range(2):
+                nc.vector.scalar_tensor_tensor(
+                    out=h[b][:, half(n)],
+                    in0=acc[b, n][:],
+                    scalar=1.0,
+                    in1=t_sb[:, b, half(n)],
+                    op0=ALU.mult,
+                    op1=ALU.add,
+                    accum_out=hs[:, n : n + 1],
+                )
+            negmu[b] = small.tile([P, 1], F32, name="negmu%d" % b)
+            nc.vector.tensor_scalar(
+                out=negmu[b][:], in0=hs[:, 0:1], scalar1=hs[:, 1:2], scalar2=-1.0 / C, op0=ALU.add, op1=ALU.mult
+            )
+
+        def variance(b):
+            sq = work.tile([P, C], BF16, tag="sq", name="sq%d" % b, bufs=1)
+            ssq = small.tile([P, 1], F32, name="ssq%d" % b)
+            nc.scalar.activation(
+                out=sq[:], in_=h[b][:], func=ACT.Square, bias=negmu[b][:], scale=1.0, accum_out=ssq[:]
+            )
+            ve = small.tile([P, 1], F32, name="ve%d" % b)
+            nc.gpsimd.tensor_scalar(out=ve[:], in0=ssq[:], scalar1=1.0 / C, scalar2=EPS, op0=ALU.mult, op1=ALU.add)
+            rstd[b] = small.tile([P, 1], F32, name="rstd%d" % b)
+            nc.gpsimd.tensor_tensor(out=rstd[b][:], in0=ve[:], in1=mhalf[:], op=ALU.pow)
+
+        def centre_times_gamma(b):
+            t1[b] = work.tile([P, C], F32, tag="t1", name="t1_%d" % b)
+            for n in range(2):
+                nc.vector.scalar_tensor_tensor(
+                    out=t1[b][:, half(n)],
+                    in0=h[b][:, half(n)],
+                    scalar=negmu[b][:],
+                    in1=gb_bc[:, 0, half(n)],
+                    op0=ALU.add,
+                    op1=ALU.mult,
+                )
+
+        def scale_shift_store(b):
+            y = work.tile([P, C], F32, tag="y", name="y%d" % b)
+            for n in range(2):
+                nc.vector.scalar_tensor_tensor(
+                    out=y[:, half(n)],
+                    in0=t1[b][:, half(n)],
+                    scalar=rstd[b][:],
+                    in1=gb_bc[:, 1, half(n)],
+                    op0=ALU.mult,
+                    op1=ALU.add,
+                )
+                nc.sync.dma_start(out=out[b, :, half(n)], in_=y[:, half(n)])
+
+        q_transpose(0)
+        k_transpose(0, 2)
+        scores(0)
+        v_regroup(0, 0)
+        row_max(0)
+        v_regroup(0, 1)
+        v_quantise(0, 0)
+        w_done = 0
+        w_quantised = 0
+        for i in range(4):
+            exponentials(i)
+            if i == 1:
+                q_transpose(1)
+            if i < 3:
+                k_transpose(i + 1, 0)
+            e_transpose(i)
+            if i < 3:
+                scores(i + 1)
+            row_sum_reciprocal(i)
+            if i > 0:
+                v_quantise(i, 0)
+            v_quantise(i, 1)
+            if i < 3:
+                v_regroup(i + 1, 0)
+                row_max(i + 1)
+            e_quantise(i)
+            if i == 3:
+                project(0, 0)
+                project(0, 1)
+                project(1, 0)
+            attend(i)
+            for j in range(W_CHUNKS_AFTER_UNIT[i]):
+                w_regroup(w_done)
+                w_done += 1
+            if i < 3:
+                v_regroup(i + 1, 1)
+                o_divide(i, 0)
+                o_divide(i, 1)
+                o_quantise(i, 0, 2)
+                while w_quantised < w_done:
+                    w_quantise(w_quantised)
+                    w_quantised += 1
+        residual_and_mean(0)
+        variance(0)
+        for g in range(2):
+            o_divide(3, g)
+            o_quantise(3, g, g + 1)
+        project(1, 1)
+        centre_times_gamma(0)
+        residual_and_mean(1)
+        variance(1)
+        scale_shift_store(0)
+        centre_times_gamma(1)
+        scale_shift_store(1)

@@ -5,7 +5,6 @@ from concourse.masks import make_identity
 
 F32 = mybir.dt.float32
 BF16 = mybir.dt.bfloat16
-I32 = mybir.dt.int32
 U32 = mybir.dt.uint32
 U8 = mybir.dt.uint8
 FP8X4 = mybir.dt.float8_e4m3fn_x4
@@ -43,10 +42,6 @@ def tile_crossattention_for_fusion_temporal_pb_kernel(tc, q, k, ki, v, vi, T, Wo
         def half(n):
             return slice(HALF * n, HALF * (n + 1))
 
-        gb_row = const.tile([P, 2 * C], BF16, name="gb_row")
-        nc.vector.memset(gb_row[:].bitcast(I32), 0)
-        ones_b = const.tile([P, P], BF16, name="ones_b")
-        nc.vector.memset(ones_b[:], 1.0)
         ident_f = const.tile([P, P], F32, name="ident_f")
         make_identity(nc, ident_f[:])
         ident_b = const.tile([P, P], BF16, name="ident_b")
@@ -60,9 +55,11 @@ def tile_crossattention_for_fusion_temporal_pb_kernel(tc, q, k, ki, v, vi, T, Wo
         w_sb = raw.tile([P, 2, 4, C], BF16, name="w_sb")
         t_sb = raw.tile([P, B, C], BF16, name="t_sb")
 
+        gb_bc = const.tile([P, 2, C], BF16, name="gb_bc")
+
         def load_gamma_beta():
-            nc.sync.dma_start(out=gb_row[0:1, 0:C], in_=gamma.rearrange("(o c) -> o c", o=1))
-            nc.sync.dma_start(out=gb_row[0:1, C : 2 * C], in_=beta.rearrange("(o c) -> o c", o=1))
+            nc.sync.dma_start(out=gb_bc[:, 0, :], in_=gamma.partition_broadcast(P))
+            nc.sync.dma_start(out=gb_bc[:, 1, :], in_=beta.partition_broadcast(P))
 
         def load_q(b):
             nc.sync.dma_start(out=q_sb[b][:], in_=q[b, :, :])
@@ -81,7 +78,6 @@ def tile_crossattention_for_fusion_temporal_pb_kernel(tc, q, k, ki, v, vi, T, Wo
         def load_t():
             nc.sync.dma_start(out=t_sb[:], in_=T.rearrange("b p c -> p b c"))
 
-        load_gamma_beta()
         load_q(0)
         load_k(0)
         load_v(0)
@@ -95,19 +91,7 @@ def tile_crossattention_for_fusion_temporal_pb_kernel(tc, q, k, ki, v, vi, T, Wo
         load_t()
         load_k(3)
         load_v(3)
-
-        gb_bc = const.tile([P, 2, C], BF16, name="gb_bc")
-        for i in range(2):
-            gp = psum.tile([P, C], BF16, tag="bank", name="gp%d" % i)
-            for n in range(2):
-                nc.tensor.matmul(
-                    out=gp[:, half(n)],
-                    lhsT=ones_b[:],
-                    rhs=gb_row[:, C * i + HALF * n : C * i + HALF * (n + 1)],
-                    start=True,
-                    stop=True,
-                )
-            nc.vector.tensor_copy(out=gb_bc[:, i, :], in_=gp[:])
+        load_gamma_beta()
 
         qT = [keep.tile([P, 4, P], F32, name="qT%d" % b) for b in range(B)]
         kT = {}
@@ -377,10 +361,11 @@ def tile_crossattention_for_fusion_temporal_pb_kernel(tc, q, k, ki, v, vi, T, Wo
                 row_max(i + 1)
             e_quantise(i)
             if i == 3:
-                project(0, 0)
-                project(0, 1)
                 project(1, 0)
             attend(i)
+            if i == 3:
+                project(0, 0)
+                project(0, 1)
             for j in range(W_CHUNKS_AFTER_UNIT[i]):
                 w_regroup(w_done)
                 w_done += 1
@@ -392,15 +377,14 @@ def tile_crossattention_for_fusion_temporal_pb_kernel(tc, q, k, ki, v, vi, T, Wo
                 while w_quantised < w_done:
                     w_quantise(w_quantised)
                     w_quantised += 1
-        residual_and_mean(0)
-        variance(0)
         for g in range(2):
             o_divide(3, g)
             o_quantise(3, g, g + 1)
         project(1, 1)
-        centre_times_gamma(0)
-        residual_and_mean(1)
-        variance(1)
-        scale_shift_store(0)
-        centre_times_gamma(1)
-        scale_shift_store(1)
+        for b in range(B):
+            residual_and_mean(b)
+            variance(b)
+        for b in range(B):
+            centre_times_gamma(b)
+        for b in range(B):
+            scale_shift_store(b)

@@ -21,7 +21,7 @@ HALF = 512
 SCALE = 1.0 / 32.0
 EPS = 1e-5
 FLOPS = 4 * (2 * P * NK * C + 2 * P * NK * DV + 2 * P * DV * C)
-W_CHUNKS_AFTER_UNIT = [1,2,1,0]
+W_CHUNKS_AFTER_UNIT = [1, 1, 2, 0]
 
 
 def tile_crossattention_for_fusion_temporal_pb_kernel(tc, q, k, ki, v, vi, T, Wout, gamma, beta, out):
@@ -87,9 +87,9 @@ def tile_crossattention_for_fusion_temporal_pb_kernel(tc, q, k, ki, v, vi, T, Wo
         load_q(1)
         load_k(2)
         load_v(2)
+        load_k(3)
         load_w(1)
         load_t()
-        load_k(3)
         load_v(3)
         load_gamma_beta()
 
@@ -100,11 +100,17 @@ def tile_crossattention_for_fusion_temporal_pb_kernel(tc, q, k, ki, v, vi, T, Wo
         e_sb = {}
         rs = {}
         rc = {}
+        rtp = {}
         eg = {}
         vg = {}
         ot = {}
         og = {}
         acc = {}
+
+        def warm_up(count):
+            scratch = psum.tile([P, P], F32, tag="bank", name="scratch")
+            for j in range(count):
+                nc.tensor.matmul(out=scratch[:], lhsT=ident_f[:], rhs=ident_f[:], start=True, stop=True)
 
         def q_transpose(b):
             tp = psum.tile([P, 4, P], F32, tag="bank", name="qtp%d" % b)
@@ -169,11 +175,10 @@ def tile_crossattention_for_fusion_temporal_pb_kernel(tc, q, k, ki, v, vi, T, Wo
         def row_sum_reciprocal(i):
             rc[i] = small.tile([P, 1], F32, name="rc%d" % i)
             nc.vector.reciprocal(out=rc[i][:], in_=rs[i][:])
-            rtp = psum.tile([P, P], F32, tag="bank", name="rtp%d" % i)
+            rtp[i] = psum.tile([P, P], F32, tag="bank", name="rtp%d" % i)
             nc.tensor.matmul(
-                out=rtp[:], lhsT=rc[i][:, 0:1].to_broadcast([P, P]), rhs=ident_f[:], start=True, stop=True
+                out=rtp[i][:], lhsT=rc[i][:, 0:1].to_broadcast([P, P]), rhs=ident_f[:], start=True, stop=True
             )
-            nc.scalar.copy(out=rt_sb[i][:], in_=rtp[:])
 
         e_codes = [keep.tile([P, P], U32, name="e_codes%d" % i, align_bytes=64) for i in range(4)]
         e_scales = [keep.tile([P, P], U8, name="e_scales%d" % i, align_bytes=64) for i in range(4)]
@@ -227,6 +232,7 @@ def tile_crossattention_for_fusion_temporal_pb_kernel(tc, q, k, ki, v, vi, T, Wo
         def o_divide(i, g):
             if g == 0:
                 og[i] = work.tile([P, 2, P, 4], BF16, tag="og", name="og%d" % i, align_bytes=64)
+                nc.vector.tensor_copy(out=rt_sb[i][:], in_=rtp[i][:])
             nc.vector.tensor_tensor(
                 out=og[i][:, g, :, :],
                 in0=ot[i, g][:].rearrange("p t m -> p m t"),
@@ -334,7 +340,9 @@ def tile_crossattention_for_fusion_temporal_pb_kernel(tc, q, k, ki, v, vi, T, Wo
                 )
                 nc.sync.dma_start(out=out[b, :, half(n)], in_=y[:, half(n)])
 
+        warm_up(6)
         q_transpose(0)
+        warm_up(6)
         k_transpose(0, 2)
         scores(0)
         v_regroup(0, 0)

@@ -10,7 +10,6 @@ U8 = mybir.dt.uint8
 FP8X4 = mybir.dt.float8_e4m3fn_x4
 ACT = mybir.ActivationFunctionType
 ALU = mybir.AluOpType
-AX = mybir.AxisListType
 
 P = 128
 B = 2
@@ -21,7 +20,9 @@ HALF = 512
 SCALE = 1.0 / 32.0
 EPS = 1e-5
 FLOPS = 4 * (2 * P * NK * C + 2 * P * NK * DV + 2 * P * DV * C)
-W_CHUNKS_AFTER_UNIT = [1, 1, 2, 0]
+W_CHUNKS_AFTER_UNIT = [1,1,1,0]
+LAST_W = "late"
+SCALAR_SHARE = [256,64,64,128]
 
 
 def tile_crossattention_for_fusion_temporal_pb_kernel(tc, q, k, ki, v, vi, T, Wout, gamma, beta, out):
@@ -102,6 +103,7 @@ def tile_crossattention_for_fusion_temporal_pb_kernel(tc, q, k, ki, v, vi, T, Wo
         rc = {}
         rtp = {}
         eg = {}
+        et = {}
         vg = {}
         ot = {}
         og = {}
@@ -151,10 +153,11 @@ def tile_crossattention_for_fusion_temporal_pb_kernel(tc, q, k, ki, v, vi, T, Wo
                     )
 
         def row_max(i):
-            mx = small.tile([P, 1], F32, name="mx%d" % i)
-            nc.vector.reduce_max(out=mx[:], in_=sc[i][:], axis=AX.X)
+            scaled = work.tile([P, NK], BF16, tag="scaled", name="scaled%d" % i, bufs=1)
             nb[i] = small.tile([P, 1], F32, name="nb%d" % i)
-            nc.vector.tensor_scalar(out=nb[i][:], in0=mx[:], scalar1=-SCALE, scalar2=None, op0=ALU.mult)
+            nc.vector.tensor_scalar(
+                out=scaled[:], in0=sc[i][:], scalar1=-SCALE, scalar2=None, op0=ALU.mult, op1=ALU.min, accum_out=nb[i][:]
+            )
 
         def exponentials(i):
             e_sb[i] = work.tile([P, NK], BF16, tag="e_sb", name="e_sb%d" % i)
@@ -163,12 +166,14 @@ def tile_crossattention_for_fusion_temporal_pb_kernel(tc, q, k, ki, v, vi, T, Wo
                 out=e_sb[i][:], in_=sc[i][:], func=ACT.Exp, bias=nb[i][:], scale=SCALE, accum_out=rs[i][:]
             )
 
-        def e_transpose(i):
-            et = psum.tile([P, 4, P], BF16, tag="bank", name="et%d" % i)
+        def e_transpose_pe(i):
+            et[i] = psum.tile([P, 4, P], BF16, tag="bank", name="et%d" % i)
             for a in range(4):
-                nc.tensor.transpose(out=et[:, a, :], in_=e_sb[i][:, P * a : P * (a + 1)], identity=ident_b[:])
+                nc.tensor.transpose(out=et[i][:, a, :], in_=e_sb[i][:, P * a : P * (a + 1)], identity=ident_b[:])
+
+        def e_copy(i):
             eg[i] = work.tile([P, P, 4], BF16, tag="eg", name="eg%d" % i, align_bytes=64)
-            nc.scalar.copy(out=eg[i][:], in_=et[:].rearrange("p a m -> p m a"))
+            nc.scalar.copy(out=eg[i][:], in_=et[i][:].rearrange("p a m -> p m a"))
 
         rt_sb = [keep.tile([P, P], F32, name="rt_sb%d" % i) for i in range(4)]
 
@@ -202,7 +207,14 @@ def tile_crossattention_for_fusion_temporal_pb_kernel(tc, q, k, ki, v, vi, T, Wo
         def v_regroup(i, h):
             if h == 0:
                 vg[i] = work.tile([P, DV, 4], BF16, tag="vg", name="vg%d" % i, align_bytes=64)
-            regroup(nc.vector.tensor_copy, vg[i][:, half(h), :], v_sb[i][:, :, half(h)])
+            cols = slice(HALF * h, HALF * (h + 1) - SCALAR_SHARE[i])
+            regroup(nc.vector.tensor_copy, vg[i][:, cols, :], v_sb[i][:, :, cols])
+
+        def v_regroup_scalar(i):
+            if SCALAR_SHARE[i]:
+                for h in range(2):
+                    cols = slice(HALF * (h + 1) - SCALAR_SHARE[i], HALF * (h + 1))
+                    regroup(nc.scalar.copy, vg[i][:, cols, :], v_sb[i][:, :, cols])
 
         def v_quantise(i, h):
             nc.vector.quantize_mx(
@@ -317,15 +329,9 @@ def tile_crossattention_for_fusion_temporal_pb_kernel(tc, q, k, ki, v, vi, T, Wo
 
         def centre_times_gamma(b):
             t1[b] = work.tile([P, C], F32, tag="t1", name="t1_%d" % b)
-            for n in range(2):
-                nc.vector.scalar_tensor_tensor(
-                    out=t1[b][:, half(n)],
-                    in0=h[b][:, half(n)],
-                    scalar=negmu[b][:],
-                    in1=gb_bc[:, 0, half(n)],
-                    op0=ALU.add,
-                    op1=ALU.mult,
-                )
+            nc.vector.scalar_tensor_tensor(
+                out=t1[b][:], in0=h[b][:], scalar=negmu[b][:], in1=gb_bc[:, 0, :], op0=ALU.add, op1=ALU.mult
+            )
 
         def scale_shift_store(b):
             y = work.tile([P, C], F32, tag="y", name="y%d" % b)
@@ -342,22 +348,30 @@ def tile_crossattention_for_fusion_temporal_pb_kernel(tc, q, k, ki, v, vi, T, Wo
 
         warm_up(6)
         q_transpose(0)
-        warm_up(6)
+        warm_up(2)
         k_transpose(0, 2)
         scores(0)
         v_regroup(0, 0)
+        v_regroup_scalar(0)
         row_max(0)
         v_regroup(0, 1)
         v_quantise(0, 0)
         w_done = 0
         w_quantised = 0
         for i in range(4):
+            if i == 3 and LAST_W == "early":
+                w_regroup(3)
             exponentials(i)
             if i == 1:
                 q_transpose(1)
             if i < 3:
                 k_transpose(i + 1, 0)
-            e_transpose(i)
+            e_transpose_pe(i)
+            if i == 3 and LAST_W == "mid":
+                w_regroup(3)
+            e_copy(i)
+            if i == 3 and LAST_W == "late":
+                w_regroup(3)
             if i < 3:
                 scores(i + 1)
             row_sum_reciprocal(i)
@@ -368,16 +382,12 @@ def tile_crossattention_for_fusion_temporal_pb_kernel(tc, q, k, ki, v, vi, T, Wo
                 v_regroup(i + 1, 0)
                 row_max(i + 1)
             e_quantise(i)
-            if i == 3:
-                project(1, 0)
             attend(i)
-            if i == 3:
-                project(0, 0)
-                project(0, 1)
             for j in range(W_CHUNKS_AFTER_UNIT[i]):
                 w_regroup(w_done)
                 w_done += 1
             if i < 3:
+                v_regroup_scalar(i + 1)
                 v_regroup(i + 1, 1)
                 o_divide(i, 0)
                 o_divide(i, 1)
@@ -385,6 +395,10 @@ def tile_crossattention_for_fusion_temporal_pb_kernel(tc, q, k, ki, v, vi, T, Wo
                 while w_quantised < w_done:
                     w_quantise(w_quantised)
                     w_quantised += 1
+        w_quantise(3)
+        for s in range(2):
+            project(0, s)
+        project(1, 0)
         for g in range(2):
             o_divide(3, g)
             o_quantise(3, g, g + 1)

@@ -20,9 +20,7 @@ HALF = 512
 SCALE = 1.0 / 32.0
 EPS = 1e-5
 FLOPS = 4 * (2 * P * NK * C + 2 * P * NK * DV + 2 * P * DV * C)
-W_CHUNKS_AFTER_UNIT = [1,1,1,0]
-LAST_W = "late"
-SCALAR_SHARE = [256,64,64,128]
+SCALAR_COLUMNS = [512,128,128,256]
 
 
 def tile_crossattention_for_fusion_temporal_pb_kernel(tc, q, k, ki, v, vi, T, Wout, gamma, beta, out):
@@ -47,20 +45,16 @@ def tile_crossattention_for_fusion_temporal_pb_kernel(tc, q, k, ki, v, vi, T, Wo
         make_identity(nc, ident_f[:])
         ident_b = const.tile([P, P], BF16, name="ident_b")
         make_identity(nc, ident_b[:])
-        mhalf = const.tile([P, 1], F32, name="mhalf")
-        nc.gpsimd.memset(mhalf[:], -0.5)
+        minus_half = const.tile([P, 1], F32, name="minus_half")
+        nc.gpsimd.memset(minus_half[:], -0.5)
 
         q_sb = [raw.tile([P, C], BF16, name="q_sb%d" % b) for b in range(B)]
         k_sb = [raw.tile([P, 4, C], BF16, name="k_sb%d" % i) for i in range(4)]
         v_sb = [raw.tile([P, 4, DV], BF16, name="v_sb%d" % i) for i in range(4)]
         w_sb = raw.tile([P, 2, 4, C], BF16, name="w_sb")
         t_sb = raw.tile([P, B, C], BF16, name="t_sb")
-
-        gb_bc = const.tile([P, 2, C], BF16, name="gb_bc")
-
-        def load_gamma_beta():
-            nc.sync.dma_start(out=gb_bc[:, 0, :], in_=gamma.partition_broadcast(P))
-            nc.sync.dma_start(out=gb_bc[:, 1, :], in_=beta.partition_broadcast(P))
+        gamma_sb = const.tile([P, C], BF16, name="gamma_sb")
+        beta_sb = const.tile([P, C], BF16, name="beta_sb")
 
         def load_q(b):
             nc.sync.dma_start(out=q_sb[b][:], in_=q[b, :, :])
@@ -76,9 +70,6 @@ def tile_crossattention_for_fusion_temporal_pb_kernel(tc, q, k, ki, v, vi, T, Wo
         def load_w(g):
             nc.sync.dma_start(out=w_sb[:, g, :, :], in_=Wout.rearrange("(g t p) n -> g p t n", g=2, t=4, p=P)[g])
 
-        def load_t():
-            nc.sync.dma_start(out=t_sb[:], in_=T.rearrange("b p c -> p b c"))
-
         load_q(0)
         load_k(0)
         load_v(0)
@@ -90,110 +81,122 @@ def tile_crossattention_for_fusion_temporal_pb_kernel(tc, q, k, ki, v, vi, T, Wo
         load_v(2)
         load_k(3)
         load_w(1)
-        load_t()
+        nc.sync.dma_start(out=t_sb[:], in_=T.rearrange("b p c -> p b c"))
         load_v(3)
-        load_gamma_beta()
-
-        qT = [keep.tile([P, 4, P], F32, name="qT%d" % b) for b in range(B)]
-        kT = {}
-        sc = {}
-        nb = {}
-        e_sb = {}
-        rs = {}
-        rc = {}
-        rtp = {}
-        eg = {}
-        et = {}
-        vg = {}
-        ot = {}
-        og = {}
-        acc = {}
+        nc.sync.dma_start(out=gamma_sb[:], in_=gamma.partition_broadcast(P))
+        nc.sync.dma_start(out=beta_sb[:], in_=beta.partition_broadcast(P))
 
         def warm_up(count):
             scratch = psum.tile([P, P], F32, tag="bank", name="scratch")
             for j in range(count):
                 nc.tensor.matmul(out=scratch[:], lhsT=ident_f[:], rhs=ident_f[:], start=True, stop=True)
 
-        def q_transpose(b):
-            tp = psum.tile([P, 4, P], F32, tag="bank", name="qtp%d" % b)
+        qT = [keep.tile([P, 4, P], F32, name="qT%d" % b) for b in range(B)]
+
+        def transpose_q(b):
+            bank = psum.tile([P, 4, P], F32, tag="bank", name="qT_ps%d" % b)
             words = q_sb[b][:].bitcast(F32)
             for u in range(4):
-                nc.tensor.transpose(out=tp[:, u, :], in_=words[:, P * u : P * (u + 1)], identity=ident_f[:])
-            nc.scalar.copy(out=qT[b][:], in_=tp[:])
+                nc.tensor.transpose(out=bank[:, u, :], in_=words[:, P * u : P * (u + 1)], identity=ident_f[:])
+            nc.scalar.copy(out=qT[b][:], in_=bank[:])
 
-        def k_transpose(i, vector_chunks):
-            kT[i] = work.tile([P, 4, NK], F32, tag="kT", name="kT%d" % i)
+        kT = {}
+
+        def transpose_k(i, vector_chunks):
             banks = []
             for u in range(4):
-                tp = psum.tile([P, 4, P], F32, tag="bank", name="ktp%d_%d" % (i, u))
+                bank = psum.tile([P, 4, P], F32, tag="bank", name="kT_ps%d_%d" % (i, u))
                 for a in range(4):
                     nc.tensor.transpose(
-                        out=tp[:, a, :],
+                        out=bank[:, a, :],
                         in_=k_sb[i][:, a, :].bitcast(F32)[:, P * u : P * (u + 1)],
                         identity=ident_f[:],
                     )
-                banks.append(tp)
+                banks.append(bank)
+            kT[i] = work.tile([P, 4, NK], F32, tag="kT", name="kT%d" % i)
             for u in range(4):
                 copy = nc.vector.tensor_copy if u >= 4 - vector_chunks else nc.scalar.copy
                 copy(out=kT[i][:, u, :], in_=banks[u][:].rearrange("p a n -> p (a n)"))
 
+        s_ps = {}
+
         def scores(i):
             b = units[i][0]
-            sc[i] = psum.tile([P, NK], F32, tag="bank", name="sc%d" % i)
+            s_ps[i] = psum.tile([P, NK], F32, tag="bank", name="s_ps%d" % i)
             for u in range(4):
                 q_pairs = qT[b][:, u, :].bitcast(BF16).rearrange("p (m e) -> p e m", e=2)
                 k_pairs = kT[i][:, u, :].bitcast(BF16).rearrange("p (n e) -> p e n", e=2)
                 for e in range(2):
                     nc.tensor.matmul(
-                        out=sc[i][:],
+                        out=s_ps[i][:],
                         lhsT=q_pairs[:, e, :],
                         rhs=k_pairs[:, e, :],
                         start=(u == 0 and e == 0),
                         stop=(u == 3 and e == 1),
                     )
 
-        def row_max(i):
+        neg_max = {}
+
+        def negative_row_max(i):
             scaled = work.tile([P, NK], BF16, tag="scaled", name="scaled%d" % i, bufs=1)
-            nb[i] = small.tile([P, 1], F32, name="nb%d" % i)
+            neg_max[i] = small.tile([P, 1], F32, name="neg_max%d" % i)
             nc.vector.tensor_scalar(
-                out=scaled[:], in0=sc[i][:], scalar1=-SCALE, scalar2=None, op0=ALU.mult, op1=ALU.min, accum_out=nb[i][:]
+                out=scaled[:],
+                in0=s_ps[i][:],
+                scalar1=-SCALE,
+                scalar2=None,
+                op0=ALU.mult,
+                op1=ALU.min,
+                accum_out=neg_max[i][:],
             )
+
+        e_sb = {}
+        row_sum = {}
 
         def exponentials(i):
             e_sb[i] = work.tile([P, NK], BF16, tag="e_sb", name="e_sb%d" % i)
-            rs[i] = small.tile([P, 1], F32, name="rs%d" % i)
+            row_sum[i] = small.tile([P, 1], F32, name="row_sum%d" % i)
             nc.scalar.activation(
-                out=e_sb[i][:], in_=sc[i][:], func=ACT.Exp, bias=nb[i][:], scale=SCALE, accum_out=rs[i][:]
+                out=e_sb[i][:],
+                in_=s_ps[i][:],
+                func=ACT.Exp,
+                bias=neg_max[i][:],
+                scale=SCALE,
+                accum_out=row_sum[i][:],
             )
 
-        def e_transpose_pe(i):
-            et[i] = psum.tile([P, 4, P], BF16, tag="bank", name="et%d" % i)
+        e_grouped = {}
+
+        def transpose_e(i):
+            bank = psum.tile([P, 4, P], BF16, tag="bank", name="eT_ps%d" % i)
             for a in range(4):
-                nc.tensor.transpose(out=et[i][:, a, :], in_=e_sb[i][:, P * a : P * (a + 1)], identity=ident_b[:])
-
-        def e_copy(i):
-            eg[i] = work.tile([P, P, 4], BF16, tag="eg", name="eg%d" % i, align_bytes=64)
-            nc.scalar.copy(out=eg[i][:], in_=et[i][:].rearrange("p a m -> p m a"))
-
-        rt_sb = [keep.tile([P, P], F32, name="rt_sb%d" % i) for i in range(4)]
-
-        def row_sum_reciprocal(i):
-            rc[i] = small.tile([P, 1], F32, name="rc%d" % i)
-            nc.vector.reciprocal(out=rc[i][:], in_=rs[i][:])
-            rtp[i] = psum.tile([P, P], F32, tag="bank", name="rtp%d" % i)
-            nc.tensor.matmul(
-                out=rtp[i][:], lhsT=rc[i][:, 0:1].to_broadcast([P, P]), rhs=ident_f[:], start=True, stop=True
-            )
+                nc.tensor.transpose(out=bank[:, a, :], in_=e_sb[i][:, P * a : P * (a + 1)], identity=ident_b[:])
+            e_grouped[i] = work.tile([P, P, 4], BF16, tag="e_grouped", name="e_grouped%d" % i, align_bytes=64)
+            nc.scalar.copy(out=e_grouped[i][:], in_=bank[:].rearrange("p a m -> p m a"))
 
         e_codes = [keep.tile([P, P], U32, name="e_codes%d" % i, align_bytes=64) for i in range(4)]
         e_scales = [keep.tile([P, P], U8, name="e_scales%d" % i, align_bytes=64) for i in range(4)]
 
-        def e_quantise(i):
+        def quantise_e(i):
             nc.vector.quantize_mx(
                 out=e_codes[i][:].bitcast(FP8X4),
                 scales=e_scales[i][:],
-                in_=eg[i][:].rearrange("p m a -> p (m a)"),
+                in_=e_grouped[i][:].rearrange("p m a -> p (m a)"),
             )
+
+        recip_ps = {}
+        recip_sb = [keep.tile([P, P], F32, name="recip_sb%d" % i) for i in range(4)]
+
+        def spread_reciprocal(i):
+            recip = small.tile([P, 1], F32, name="recip%d" % i)
+            nc.vector.reciprocal(out=recip[:], in_=row_sum[i][:])
+            recip_ps[i] = psum.tile([P, P], F32, tag="bank", name="recip_ps%d" % i)
+            nc.tensor.matmul(
+                out=recip_ps[i][:], lhsT=recip[:, 0:1].to_broadcast([P, P]), rhs=ident_f[:], start=True, stop=True
+            )
+
+        def copy_reciprocal(i):
+            nc.vector.tensor_copy(out=recip_sb[i][:], in_=recip_ps[i][:])
 
         def regroup(copy, dst, src):
             copy(
@@ -201,38 +204,39 @@ def tile_crossattention_for_fusion_temporal_pb_kernel(tc, q, k, ki, v, vi, T, Wo
                 in_=src.rearrange("p t (c i) -> p c t i", i=4),
             )
 
+        v_grouped = {}
         v_codes = [keep.tile([P, DV], U32, name="v_codes%d" % i, align_bytes=64) for i in range(4)]
         v_scales = [keep.tile([P, DV], U8, name="v_scales%d" % i, align_bytes=64) for i in range(4)]
 
-        def v_regroup(i, h):
-            if h == 0:
-                vg[i] = work.tile([P, DV, 4], BF16, tag="vg", name="vg%d" % i, align_bytes=64)
-            cols = slice(HALF * h, HALF * (h + 1) - SCALAR_SHARE[i])
-            regroup(nc.vector.tensor_copy, vg[i][:, cols, :], v_sb[i][:, :, cols])
+        def regroup_v_first_half(i):
+            v_grouped[i] = work.tile([P, DV, 4], BF16, tag="v_grouped", name="v_grouped%d" % i, align_bytes=64)
+            regroup(nc.vector.tensor_copy, v_grouped[i][:, half(0), :], v_sb[i][:, :, half(0)])
 
-        def v_regroup_scalar(i):
-            if SCALAR_SHARE[i]:
-                for h in range(2):
-                    cols = slice(HALF * (h + 1) - SCALAR_SHARE[i], HALF * (h + 1))
-                    regroup(nc.scalar.copy, vg[i][:, cols, :], v_sb[i][:, :, cols])
+        def regroup_v_second_half(i):
+            cut = DV - SCALAR_COLUMNS[i]
+            if cut > HALF:
+                regroup(nc.vector.tensor_copy, v_grouped[i][:, HALF:cut, :], v_sb[i][:, :, HALF:cut])
 
-        def v_quantise(i, h):
+        def regroup_v_on_scalar(i):
+            cut = DV - SCALAR_COLUMNS[i]
+            regroup(nc.scalar.copy, v_grouped[i][:, cut:DV, :], v_sb[i][:, :, cut:DV])
+
+        def quantise_v(i, n):
             nc.vector.quantize_mx(
-                out=v_codes[i][:, half(h)].bitcast(FP8X4),
-                scales=v_scales[i][:, half(h)],
-                in_=vg[i][:, half(h), :].rearrange("p w j -> p (w j)"),
+                out=v_codes[i][:, half(n)].bitcast(FP8X4),
+                scales=v_scales[i][:, half(n)],
+                in_=v_grouped[i][:, half(n), :].rearrange("p w j -> p (w j)"),
             )
 
-        o_codes = [keep.tile([P, 2 * P], U32, name="o_codes%d" % i, align_bytes=64) for i in range(4)]
-        o_scales = [keep.tile([P, 2 * P], U8, name="o_scales%d" % i, align_bytes=64) for i in range(4)]
+        oT_ps = {}
 
         def attend(i):
             for g in range(2):
-                ot[i, g] = psum.tile([P, 4, P], F32, tag="bank", name="ot%d_%d" % (i, g))
+                oT_ps[i, g] = psum.tile([P, 4, P], F32, tag="bank", name="oT_ps%d_%d" % (i, g))
                 for t in range(4):
                     cols = slice(P * (4 * g + t), P * (4 * g + t + 1))
                     nc.tensor.matmul_mx(
-                        out=ot[i, g][:, t, :],
+                        out=oT_ps[i, g][:, t, :],
                         lhsT=v_codes[i][:, cols].bitcast(FP8X4),
                         lhsT_scale=v_scales[i][:, cols],
                         rhs=e_codes[i][:].bitcast(FP8X4),
@@ -241,96 +245,115 @@ def tile_crossattention_for_fusion_temporal_pb_kernel(tc, q, k, ki, v, vi, T, Wo
                         stop=True,
                     )
 
-        def o_divide(i, g):
-            if g == 0:
-                og[i] = work.tile([P, 2, P, 4], BF16, tag="og", name="og%d" % i, align_bytes=64)
-                nc.vector.tensor_copy(out=rt_sb[i][:], in_=rtp[i][:])
-            nc.vector.tensor_tensor(
-                out=og[i][:, g, :, :],
-                in0=ot[i, g][:].rearrange("p t m -> p m t"),
-                in1=rt_sb[i][:].unsqueeze(2).to_broadcast([P, P, 4]),
-                op=ALU.mult,
-            )
+        o_grouped = {}
+        o_codes = [keep.tile([P, 2 * P], U32, name="o_codes%d" % i, align_bytes=64) for i in range(4)]
+        o_scales = [keep.tile([P, 2 * P], U8, name="o_scales%d" % i, align_bytes=64) for i in range(4)]
 
-        def o_quantise(i, g0, g1):
-            cols = slice(P * g0, P * g1)
+        def divide_o(i):
+            o_grouped[i] = work.tile([P, 2, P, 4], BF16, tag="o_grouped", name="o_grouped%d" % i, align_bytes=64)
+            for g in range(2):
+                nc.vector.tensor_tensor(
+                    out=o_grouped[i][:, g, :, :],
+                    in0=oT_ps[i, g][:].rearrange("p t m -> p m t"),
+                    in1=recip_sb[i][:].unsqueeze(2).to_broadcast([P, P, 4]),
+                    op=ALU.mult,
+                )
+
+        def quantise_o(i):
             nc.vector.quantize_mx(
-                out=o_codes[i][:, cols].bitcast(FP8X4),
-                scales=o_scales[i][:, cols],
-                in_=og[i][:, g0:g1, :, :].rearrange("p g m t -> p (g m t)"),
+                out=o_codes[i][:].bitcast(FP8X4),
+                scales=o_scales[i][:],
+                in_=o_grouped[i][:].rearrange("p g m t -> p (g m t)"),
             )
 
+        w_grouped = keep.tile([P, 2, C, 4], BF16, name="w_grouped", align_bytes=64)
         w_codes = keep.tile([P, 2, C], U32, name="w_codes", align_bytes=64)
         w_scales = keep.tile([P, 2, C], U8, name="w_scales", align_bytes=64)
-        wg = keep.tile([P, 2, C, 4], BF16, name="wg", align_bytes=64)
 
-        def w_regroup(j):
+        def regroup_w(j):
             g, n = divmod(j, 2)
-            regroup(nc.scalar.copy, wg[:, g, half(n), :], w_sb[:, g, :, half(n)])
+            regroup(nc.scalar.copy, w_grouped[:, g, half(n), :], w_sb[:, g, :, half(n)])
 
-        def w_quantise(j):
+        def quantise_w(j):
             g, n = divmod(j, 2)
             nc.vector.quantize_mx(
                 out=w_codes[:, g, half(n)].bitcast(FP8X4),
                 scales=w_scales[:, g, half(n)],
-                in_=wg[:, g, half(n), :].rearrange("p w j -> p (w j)"),
+                in_=w_grouped[:, g, half(n), :].rearrange("p w j -> p (w j)"),
             )
 
-        def project(b, s):
-            i = 2 * b + s
-            for g in range(2):
-                rows = slice(P * g, P * (g + 1))
-                for n in range(2):
-                    if s == 0 and g == 0:
-                        acc[b, n] = psum.tile([P, HALF], F32, tag="bank", name="acc%d_%d" % (b, n))
-                    nc.tensor.matmul_mx(
-                        out=acc[b, n][:],
-                        lhsT=o_codes[i][:, rows].bitcast(FP8X4),
-                        lhsT_scale=o_scales[i][:, rows],
-                        rhs=w_codes[:, g, half(n)].bitcast(FP8X4),
-                        rhs_scale=w_scales[:, g, half(n)],
-                        start=(s == 0 and g == 0),
-                        stop=(s == 1 and g == 1),
-                    )
+        x_ps = {}
 
-        h = {}
-        negmu = {}
-        t1 = {}
+        def project(b, s, chunks):
+            i = 2 * b + s
+            for j in chunks:
+                g, n = divmod(j, 2)
+                if s == 0 and g == 0:
+                    x_ps[b, n] = psum.tile([P, HALF], F32, tag="bank", name="x_ps%d_%d" % (b, n))
+                rows = slice(P * g, P * (g + 1))
+                nc.tensor.matmul_mx(
+                    out=x_ps[b, n][:],
+                    lhsT=o_codes[i][:, rows].bitcast(FP8X4),
+                    lhsT_scale=o_scales[i][:, rows],
+                    rhs=w_codes[:, g, half(n)].bitcast(FP8X4),
+                    rhs_scale=w_scales[:, g, half(n)],
+                    start=(s == 0 and g == 0),
+                    stop=(s == 1 and g == 1),
+                )
+
+        hidden = {}
+        half_sums = {}
+        neg_mean = {}
+        centred = {}
         rstd = {}
 
-        def residual_and_mean(b):
-            h[b] = work.tile([P, C], F32, tag="h", name="h%d" % b)
-            hs = small.tile([P, 2], F32, name="hs%d" % b)
-            for n in range(2):
-                nc.vector.scalar_tensor_tensor(
-                    out=h[b][:, half(n)],
-                    in0=acc[b, n][:],
-                    scalar=1.0,
-                    in1=t_sb[:, b, half(n)],
-                    op0=ALU.mult,
-                    op1=ALU.add,
-                    accum_out=hs[:, n : n + 1],
-                )
-            negmu[b] = small.tile([P, 1], F32, name="negmu%d" % b)
+        def residual(b, n):
+            if n == 0:
+                hidden[b] = work.tile([P, C], F32, tag="hidden", name="hidden%d" % b)
+                half_sums[b] = small.tile([P, 2], F32, name="half_sums%d" % b)
+            nc.vector.scalar_tensor_tensor(
+                out=hidden[b][:, half(n)],
+                in0=x_ps[b, n][:],
+                scalar=1.0,
+                in1=t_sb[:, b, half(n)],
+                op0=ALU.mult,
+                op1=ALU.add,
+                accum_out=half_sums[b][:, n : n + 1],
+            )
+
+        def mean(b):
+            neg_mean[b] = small.tile([P, 1], F32, name="neg_mean%d" % b)
             nc.vector.tensor_scalar(
-                out=negmu[b][:], in0=hs[:, 0:1], scalar1=hs[:, 1:2], scalar2=-1.0 / C, op0=ALU.add, op1=ALU.mult
+                out=neg_mean[b][:],
+                in0=half_sums[b][:, 0:1],
+                scalar1=half_sums[b][:, 1:2],
+                scalar2=-1.0 / C,
+                op0=ALU.add,
+                op1=ALU.mult,
             )
 
         def variance(b):
-            sq = work.tile([P, C], BF16, tag="sq", name="sq%d" % b, bufs=1)
-            ssq = small.tile([P, 1], F32, name="ssq%d" % b)
+            squares = work.tile([P, C], BF16, tag="squares", name="squares%d" % b, bufs=1)
+            square_sum = small.tile([P, 1], F32, name="square_sum%d" % b)
             nc.scalar.activation(
-                out=sq[:], in_=h[b][:], func=ACT.Square, bias=negmu[b][:], scale=1.0, accum_out=ssq[:]
+                out=squares[:],
+                in_=hidden[b][:],
+                func=ACT.Square,
+                bias=neg_mean[b][:],
+                scale=1.0,
+                accum_out=square_sum[:],
             )
-            ve = small.tile([P, 1], F32, name="ve%d" % b)
-            nc.gpsimd.tensor_scalar(out=ve[:], in0=ssq[:], scalar1=1.0 / C, scalar2=EPS, op0=ALU.mult, op1=ALU.add)
+            var_eps = small.tile([P, 1], F32, name="var_eps%d" % b)
+            nc.gpsimd.tensor_scalar(
+                out=var_eps[:], in0=square_sum[:], scalar1=1.0 / C, scalar2=EPS, op0=ALU.mult, op1=ALU.add
+            )
             rstd[b] = small.tile([P, 1], F32, name="rstd%d" % b)
-            nc.gpsimd.tensor_tensor(out=rstd[b][:], in0=ve[:], in1=mhalf[:], op=ALU.pow)
+            nc.gpsimd.tensor_tensor(out=rstd[b][:], in0=var_eps[:], in1=minus_half[:], op=ALU.pow)
 
         def centre_times_gamma(b):
-            t1[b] = work.tile([P, C], F32, tag="t1", name="t1_%d" % b)
+            centred[b] = work.tile([P, C], F32, tag="centred", name="centred%d" % b)
             nc.vector.scalar_tensor_tensor(
-                out=t1[b][:], in0=h[b][:], scalar=negmu[b][:], in1=gb_bc[:, 0, :], op0=ALU.add, op1=ALU.mult
+                out=centred[b][:], in0=hidden[b][:], scalar=neg_mean[b][:], in1=gamma_sb[:], op0=ALU.add, op1=ALU.mult
             )
 
         def scale_shift_store(b):
@@ -338,74 +361,65 @@ def tile_crossattention_for_fusion_temporal_pb_kernel(tc, q, k, ki, v, vi, T, Wo
             for n in range(2):
                 nc.vector.scalar_tensor_tensor(
                     out=y[:, half(n)],
-                    in0=t1[b][:, half(n)],
+                    in0=centred[b][:, half(n)],
                     scalar=rstd[b][:],
-                    in1=gb_bc[:, 1, half(n)],
+                    in1=beta_sb[:, half(n)],
                     op0=ALU.mult,
                     op1=ALU.add,
                 )
                 nc.sync.dma_start(out=out[b, :, half(n)], in_=y[:, half(n)])
 
         warm_up(6)
-        q_transpose(0)
+        transpose_q(0)
         warm_up(2)
-        k_transpose(0, 2)
+        transpose_k(0, 2)
         scores(0)
-        v_regroup(0, 0)
-        v_regroup_scalar(0)
-        row_max(0)
-        v_regroup(0, 1)
-        v_quantise(0, 0)
-        w_done = 0
-        w_quantised = 0
+        regroup_v_first_half(0)
+        regroup_v_on_scalar(0)
+        negative_row_max(0)
+        regroup_v_second_half(0)
         for i in range(4):
-            if i == 3 and LAST_W == "early":
-                w_regroup(3)
+            last = i == 3
             exponentials(i)
             if i == 1:
-                q_transpose(1)
-            if i < 3:
-                k_transpose(i + 1, 0)
-            e_transpose_pe(i)
-            if i == 3 and LAST_W == "mid":
-                w_regroup(3)
-            e_copy(i)
-            if i == 3 and LAST_W == "late":
-                w_regroup(3)
-            if i < 3:
+                transpose_q(1)
+            if not last:
+                transpose_k(i + 1, 0)
+            transpose_e(i)
+            if not last:
                 scores(i + 1)
-            row_sum_reciprocal(i)
-            if i > 0:
-                v_quantise(i, 0)
-            v_quantise(i, 1)
-            if i < 3:
-                v_regroup(i + 1, 0)
-                row_max(i + 1)
-            e_quantise(i)
+            spread_reciprocal(i)
+            regroup_w(i)
+            quantise_v(i, 0)
+            quantise_v(i, 1)
+            if not last:
+                regroup_v_first_half(i + 1)
+                regroup_v_on_scalar(i + 1)
+                negative_row_max(i + 1)
+            quantise_e(i)
+            if last:
+                project(0, 0, (0, 1, 2))
+                project(0, 1, (0, 1, 2))
             attend(i)
-            for j in range(W_CHUNKS_AFTER_UNIT[i]):
-                w_regroup(w_done)
-                w_done += 1
-            if i < 3:
-                v_regroup_scalar(i + 1)
-                v_regroup(i + 1, 1)
-                o_divide(i, 0)
-                o_divide(i, 1)
-                o_quantise(i, 0, 2)
-                while w_quantised < w_done:
-                    w_quantise(w_quantised)
-                    w_quantised += 1
-        w_quantise(3)
-        for s in range(2):
-            project(0, s)
-        project(1, 0)
-        for g in range(2):
-            o_divide(3, g)
-            o_quantise(3, g, g + 1)
-        project(1, 1)
-        for b in range(B):
-            residual_and_mean(b)
-            variance(b)
+            if last:
+                project(1, 0, (0, 1, 2))
+            copy_reciprocal(i)
+            if not last:
+                regroup_v_second_half(i + 1)
+            divide_o(i)
+            quantise_w(i)
+            quantise_o(i)
+        for b, s in units[:3]:
+            project(b, s, (3,))
+        project(1, 1, (0, 1, 2, 3))
+        residual(0, 0)
+        residual(0, 1)
+        residual(1, 0)
+        mean(0)
+        variance(0)
+        residual(1, 1)
+        mean(1)
+        variance(1)
         for b in range(B):
             centre_times_gamma(b)
         for b in range(B):

@@ -385,6 +385,7 @@ def tile_crossattention_for_fusion_temporal_pb_kernel(tc, q, k, ki, v, vi, T, Wo
                 transpose_q(1)
             if not last:
                 transpose_k(i + 1, 0)
+                warm_up(2)
             transpose_e(i)
             if not last:
                 scores(i + 1)

@@ -371,7 +371,7 @@ def tile_crossattention_for_fusion_temporal_pb_kernel(tc, q, k, ki, v, vi, T, Wo
 
         warm_up(6)
         transpose_q(0)
-        warm_up(2)
+        warm_up(6)
         transpose_k(0, 2)
         scores(0)
         regroup_v_first_half(0)
@@ -385,7 +385,6 @@ def tile_crossattention_for_fusion_temporal_pb_kernel(tc, q, k, ki, v, vi, T, Wo
                 transpose_q(1)
             if not last:
                 transpose_k(i + 1, 0)
-                warm_up(2)
             transpose_e(i)
             if not last:
                 scores(i + 1)

@@ -20,7 +20,7 @@ HALF = 512
 SCALE = 1.0 / 32.0
 EPS = 1e-5
 FLOPS = 4 * (2 * P * NK * C + 2 * P * NK * DV + 2 * P * DV * C)
-SCALAR_COLUMNS = [512,128,128,256]
+V0_HALVES = True
 
 
 def tile_crossattention_for_fusion_temporal_pb_kernel(tc, q, k, ki, v, vi, T, Wout, gamma, beta, out):
@@ -43,15 +43,15 @@ def tile_crossattention_for_fusion_temporal_pb_kernel(tc, q, k, ki, v, vi, T, Wo
 
         ident_f = const.tile([P, P], F32, name="ident_f")
         make_identity(nc, ident_f[:])
-        ident_b = const.tile([P, P], BF16, name="ident_b")
-        make_identity(nc, ident_b[:])
         minus_half = const.tile([P, 1], F32, name="minus_half")
         nc.gpsimd.memset(minus_half[:], -0.5)
 
         q_sb = [raw.tile([P, C], BF16, name="q_sb%d" % b) for b in range(B)]
         k_sb = [raw.tile([P, 4, C], BF16, name="k_sb%d" % i) for i in range(4)]
         v_sb = [raw.tile([P, 4, DV], BF16, name="v_sb%d" % i) for i in range(4)]
-        w_sb = raw.tile([P, 2, 4, C], BF16, name="w_sb")
+        w_sb = [raw.tile([P, 4, HALF], BF16, name="w_sb%d" % j) for j in range(2)]
+        w_sb1 = raw.tile([P, 4, C], BF16, name="w_sb_last")
+        v_half_sb = [raw.tile([P, 4, HALF], BF16, name="v_half_sb%d" % n) for n in range(2)]
         t_sb = raw.tile([P, B, C], BF16, name="t_sb")
         gamma_sb = const.tile([P, C], BF16, name="gamma_sb")
         beta_sb = const.tile([P, C], BF16, name="beta_sb")
@@ -63,28 +63,34 @@ def tile_crossattention_for_fusion_temporal_pb_kernel(tc, q, k, ki, v, vi, T, Wo
             b, s = units[i]
             nc.sync.dma_start(out=k_sb[i][:], in_=key_src[s][b, :, :].rearrange("(p a) c -> p a c", a=4))
 
+        def load_k_rows(i, a):
+            b, s = units[i]
+            nc.sync.dma_start(out=k_sb[i][:, a, :], in_=key_src[s][b, P * a : P * (a + 1), :])
+
+        def load_v_half(i, n):
+            b, s = units[i]
+            nc.sync.dma_start(
+                out=v_half_sb[n][:],
+                in_=val_src[s][b, :, half(n)].rearrange("(p j) w -> p j w", j=4),
+            )
+
         def load_v(i):
             b, s = units[i]
             nc.sync.dma_start(out=v_sb[i][:], in_=val_src[s][b, :, :].rearrange("(p j) w -> p j w", j=4))
 
-        def load_w(g):
-            nc.sync.dma_start(out=w_sb[:, g, :, :], in_=Wout.rearrange("(g t p) n -> g p t n", g=2, t=4, p=P)[g])
+        def load_rest():
+            load_t()
+            load_gb()
 
-        load_q(0)
-        load_k(0)
-        load_v(0)
-        load_k(1)
-        load_v(1)
-        load_w(0)
-        load_q(1)
-        load_k(2)
-        load_v(2)
-        load_k(3)
-        load_w(1)
-        nc.sync.dma_start(out=t_sb[:], in_=T.rearrange("b p c -> p b c"))
-        load_v(3)
-        nc.sync.dma_start(out=gamma_sb[:], in_=gamma.partition_broadcast(P))
-        nc.sync.dma_start(out=beta_sb[:], in_=beta.partition_broadcast(P))
+        def load_t():
+            nc.sync.dma_start(out=t_sb[:], in_=T.rearrange("b p c -> p b c"))
+
+        def load_gb():
+            nc.sync.dma_start(out=gamma_sb[:], in_=gamma.partition_broadcast(P))
+            nc.sync.dma_start(out=beta_sb[:], in_=beta.partition_broadcast(P))
+
+        def load_w(g):
+            nc.sync.dma_start(out=w_sb1[:], in_=Wout.rearrange("(g t p) n -> g p t n", g=2, t=4, p=P)[1])
 
         def warm_up(count):
             scratch = psum.tile([P, P], F32, tag="bank", name="scratch")
@@ -93,12 +99,12 @@ def tile_crossattention_for_fusion_temporal_pb_kernel(tc, q, k, ki, v, vi, T, Wo
 
         qT = [keep.tile([P, 4, P], F32, name="qT%d" % b) for b in range(B)]
 
-        def transpose_q(b):
+        def transpose_q(b, copy=nc.scalar.copy):
             bank = psum.tile([P, 4, P], F32, tag="bank", name="qT_ps%d" % b)
             words = q_sb[b][:].bitcast(F32)
             for u in range(4):
                 nc.tensor.transpose(out=bank[:, u, :], in_=words[:, P * u : P * (u + 1)], identity=ident_f[:])
-            nc.scalar.copy(out=qT[b][:], in_=bank[:])
+            copy(out=qT[b][:], in_=bank[:])
 
         kT = {}
 
@@ -116,7 +122,19 @@ def tile_crossattention_for_fusion_temporal_pb_kernel(tc, q, k, ki, v, vi, T, Wo
             kT[i] = work.tile([P, 4, NK], F32, tag="kT", name="kT%d" % i)
             for u in range(4):
                 copy = nc.vector.tensor_copy if u >= 4 - vector_chunks else nc.scalar.copy
-                copy(out=kT[i][:, u, :], in_=banks[u][:].rearrange("p a n -> p (a n)"))
+                copy(
+                    out=kT[i][:, u, :].rearrange("p (n a) -> p n a", a=4),
+                    in_=banks[u][:].rearrange("p a n -> p n a"),
+                )
+
+        def transpose_k_rows(i, a, copy):
+            if i not in kT:
+                kT[i] = work.tile([P, 4, NK], F32, tag="kT", name="kT%d" % i)
+            bank = psum.tile([P, 4, P], F32, tag="bank", name="kTr_ps%d_%d" % (i, a))
+            words = k_sb[i][:, a, :].bitcast(F32)
+            for u in range(4):
+                nc.tensor.transpose(out=bank[:, u, :], in_=words[:, P * u : P * (u + 1)], identity=ident_f[:])
+            copy(out=kT[i][:, a, :], in_=bank[:].rearrange("p u n -> p (u n)"))
 
         s_ps = {}
 
@@ -134,6 +152,22 @@ def tile_crossattention_for_fusion_temporal_pb_kernel(tc, q, k, ki, v, vi, T, Wo
                         start=(u == 0 and e == 0),
                         stop=(u == 3 and e == 1),
                     )
+
+        def scores_by_rows(i):
+            b = units[i][0]
+            s_ps[i] = psum.tile([P, NK], F32, tag="bank", name="s_ps%d" % i)
+            for a in range(4):
+                for u in range(4):
+                    q_pairs = qT[b][:, u, :].bitcast(BF16).rearrange("p (m e) -> p e m", e=2)
+                    k_pairs = kT[i][:, a, P * u : P * (u + 1)].bitcast(BF16).rearrange("p (n e) -> p e n", e=2)
+                    for e in range(2):
+                        nc.tensor.matmul(
+                            out=s_ps[i][:, P * a : P * (a + 1)],
+                            lhsT=q_pairs[:, e, :],
+                            rhs=k_pairs[:, e, :],
+                            start=(u == 0 and e == 0),
+                            stop=(u == 3 and e == 1),
+                        )
 
         neg_max = {}
 
@@ -168,11 +202,15 @@ def tile_crossattention_for_fusion_temporal_pb_kernel(tc, q, k, ki, v, vi, T, Wo
         e_grouped = {}
 
         def transpose_e(i):
-            bank = psum.tile([P, 4, P], BF16, tag="bank", name="eT_ps%d" % i)
-            for a in range(4):
-                nc.tensor.transpose(out=bank[:, a, :], in_=e_sb[i][:, P * a : P * (a + 1)], identity=ident_b[:])
-            e_grouped[i] = work.tile([P, P, 4], BF16, tag="e_grouped", name="e_grouped%d" % i, align_bytes=64)
-            nc.scalar.copy(out=e_grouped[i][:], in_=bank[:].rearrange("p a m -> p m a"))
+            bank = psum.tile([P, 2, P], F32, tag="bank", name="eT_ps%d" % i)
+            words = e_sb[i][:].bitcast(F32)
+            for h in range(2):
+                nc.tensor.transpose(out=bank[:, h, :], in_=words[:, h : 2 * P : 2], identity=ident_f[:])
+            e_grouped[i] = work.tile([P, P * 4], BF16, tag="e_grouped", name="e_grouped%d" % i, align_bytes=64)
+            nc.scalar.copy(
+                out=e_grouped[i][:].bitcast(F32).rearrange("p (m h) -> p m h", h=2),
+                in_=bank[:].rearrange("p h m -> p m h"),
+            )
 
         e_codes = [keep.tile([P, P], U32, name="e_codes%d" % i, align_bytes=64) for i in range(4)]
         e_scales = [keep.tile([P, P], U8, name="e_scales%d" % i, align_bytes=64) for i in range(4)]
@@ -181,18 +219,22 @@ def tile_crossattention_for_fusion_temporal_pb_kernel(tc, q, k, ki, v, vi, T, Wo
             nc.vector.quantize_mx(
                 out=e_codes[i][:].bitcast(FP8X4),
                 scales=e_scales[i][:],
-                in_=e_grouped[i][:].rearrange("p m a -> p (m a)"),
+                in_=e_grouped[i][:],
             )
 
         recip_ps = {}
         recip_sb = [keep.tile([P, P], F32, name="recip_sb%d" % i) for i in range(4)]
 
+        recip = {}
+
+        def reciprocal(i):
+            recip[i] = small.tile([P, 1], F32, name="recip%d" % i)
+            nc.vector.reciprocal(out=recip[i][:], in_=row_sum[i][:])
+
         def spread_reciprocal(i):
-            recip = small.tile([P, 1], F32, name="recip%d" % i)
-            nc.vector.reciprocal(out=recip[:], in_=row_sum[i][:])
             recip_ps[i] = psum.tile([P, P], F32, tag="bank", name="recip_ps%d" % i)
             nc.tensor.matmul(
-                out=recip_ps[i][:], lhsT=recip[:, 0:1].to_broadcast([P, P]), rhs=ident_f[:], start=True, stop=True
+                out=recip_ps[i][:], lhsT=recip[i][:, 0:1].to_broadcast([P, P]), rhs=ident_f[:], start=True, stop=True
             )
 
         def copy_reciprocal(i):
@@ -208,18 +250,14 @@ def tile_crossattention_for_fusion_temporal_pb_kernel(tc, q, k, ki, v, vi, T, Wo
         v_codes = [keep.tile([P, DV], U32, name="v_codes%d" % i, align_bytes=64) for i in range(4)]
         v_scales = [keep.tile([P, DV], U8, name="v_scales%d" % i, align_bytes=64) for i in range(4)]
 
-        def regroup_v_first_half(i):
-            v_grouped[i] = work.tile([P, DV, 4], BF16, tag="v_grouped", name="v_grouped%d" % i, align_bytes=64)
-            regroup(nc.vector.tensor_copy, v_grouped[i][:, half(0), :], v_sb[i][:, :, half(0)])
-
-        def regroup_v_second_half(i):
-            cut = DV - SCALAR_COLUMNS[i]
-            if cut > HALF:
-                regroup(nc.vector.tensor_copy, v_grouped[i][:, HALF:cut, :], v_sb[i][:, :, HALF:cut])
-
-        def regroup_v_on_scalar(i):
-            cut = DV - SCALAR_COLUMNS[i]
-            regroup(nc.scalar.copy, v_grouped[i][:, cut:DV, :], v_sb[i][:, :, cut:DV])
+        def regroup_v(copy, i, lo, hi):
+            if i not in v_grouped:
+                v_grouped[i] = work.tile([P, DV, 4], BF16, tag="v_grouped", name="v_grouped%d" % i, align_bytes=64)
+            src = v_sb[i][:, :, lo:hi]
+            if i == 0 and V0_HALVES:
+                n = lo // HALF
+                src = v_half_sb[n][:, :, lo - HALF * n : hi - HALF * n]
+            regroup(copy, v_grouped[i][:, lo:hi, :], src)
 
         def quantise_v(i, n):
             nc.vector.quantize_mx(
@@ -244,6 +282,19 @@ def tile_crossattention_for_fusion_temporal_pb_kernel(tc, q, k, ki, v, vi, T, Wo
                         start=True,
                         stop=True,
                     )
+
+        def keep_warm(i, count):
+            scratch = psum.tile([P, HALF], F32, tag="bank", name="warm_ps%d" % i)
+            for j in range(count):
+                nc.tensor.matmul_mx(
+                    out=scratch[:],
+                    lhsT=e_codes[i][:].bitcast(FP8X4),
+                    lhsT_scale=e_scales[i][:],
+                    rhs=v_codes[i][:, half(j % 2)].bitcast(FP8X4),
+                    rhs_scale=v_scales[i][:, half(j % 2)],
+                    start=True,
+                    stop=True,
+                )
 
         o_grouped = {}
         o_codes = [keep.tile([P, 2 * P], U32, name="o_codes%d" % i, align_bytes=64) for i in range(4)]
@@ -270,9 +321,15 @@ def tile_crossattention_for_fusion_temporal_pb_kernel(tc, q, k, ki, v, vi, T, Wo
         w_codes = keep.tile([P, 2, C], U32, name="w_codes", align_bytes=64)
         w_scales = keep.tile([P, 2, C], U8, name="w_scales", align_bytes=64)
 
-        def regroup_w(j):
+        def load_w_half(g, n):
+            nc.sync.dma_start(
+                out=w_sb[n][:] if g == 0 else w_sb1[:, :, half(n)],
+                in_=Wout.rearrange("(g t p) n -> g p t n", g=2, t=4, p=P)[g][:, :, half(n)],
+            )
+
+        def regroup_w(j, copy=nc.scalar.copy):
             g, n = divmod(j, 2)
-            regroup(nc.scalar.copy, w_grouped[:, g, half(n), :], w_sb[:, g, :, half(n)])
+            regroup(copy, w_grouped[:, g, half(n), :], w_sb[n][:] if g == 0 else w_sb1[:, :, half(n)])
 
         def quantise_w(j):
             g, n = divmod(j, 2)
@@ -356,71 +413,141 @@ def tile_crossattention_for_fusion_temporal_pb_kernel(tc, q, k, ki, v, vi, T, Wo
                 out=centred[b][:], in0=hidden[b][:], scalar=neg_mean[b][:], in1=gamma_sb[:], op0=ALU.add, op1=ALU.mult
             )
 
-        def scale_shift_store(b):
-            y = work.tile([P, C], F32, tag="y", name="y%d" % b)
-            for n in range(2):
-                nc.vector.scalar_tensor_tensor(
-                    out=y[:, half(n)],
-                    in0=centred[b][:, half(n)],
-                    scalar=rstd[b][:],
-                    in1=beta_sb[:, half(n)],
-                    op0=ALU.mult,
-                    op1=ALU.add,
-                )
-                nc.sync.dma_start(out=out[b, :, half(n)], in_=y[:, half(n)])
+        y = {}
 
+        def scale_shift_store(b, n):
+            if b not in y:
+                y[b] = work.tile([P, C], F32, tag="y", name="y%d" % b)
+            nc.vector.scalar_tensor_tensor(
+                out=y[b][:, half(n)],
+                in0=centred[b][:, half(n)],
+                scalar=rstd[b][:],
+                in1=beta_sb[:, half(n)],
+                op0=ALU.mult,
+                op1=ALU.add,
+            )
+            nc.sync.dma_start(out=out[b, :, half(n)], in_=y[b][:, half(n)])
+
+        V = nc.vector.tensor_copy
+        S = nc.scalar.copy
+        load_w_half(0, 0)
+        load_q(0)
+        load_k_rows(0, 0)
+        load_k_rows(0, 1)
+        load_k_rows(0, 2)
+        load_k_rows(0, 3)
+        load_v_half(0, 0)
+        load_v_half(0, 1)
+        load_k(1)
+        load_v(1)
+        load_w_half(0, 1)
+        load_q(1)
+        load_k(2)
+        load_v(2)
+        load_w(1)
+        load_k(3)
+        load_v(3)
+        load_t()
+        load_gb()
         warm_up(6)
-        transpose_q(0)
-        warm_up(6)
-        transpose_k(0, 2)
-        scores(0)
-        regroup_v_first_half(0)
-        regroup_v_on_scalar(0)
+        warm_up(2)
+        regroup_w(0, V)
+        quantise_w(0)
+        transpose_q(0, S)
+        transpose_k_rows(0, 0, S)
+        transpose_k_rows(0, 1, V)
+        warm_up(2)
+        transpose_k_rows(0, 2, S)
+        transpose_k_rows(0, 3, V)
+        scores_by_rows(0)
+        regroup_v(V, 0, 0, 512)
+        regroup_v(S, 0, 512, 1024)
         negative_row_max(0)
-        regroup_v_second_half(0)
-        for i in range(4):
-            last = i == 3
-            exponentials(i)
-            if i == 1:
-                transpose_q(1)
-            if not last:
-                transpose_k(i + 1, 0)
-            transpose_e(i)
-            if not last:
-                scores(i + 1)
-            spread_reciprocal(i)
-            regroup_w(i)
-            quantise_v(i, 0)
-            quantise_v(i, 1)
-            if not last:
-                regroup_v_first_half(i + 1)
-                regroup_v_on_scalar(i + 1)
-                negative_row_max(i + 1)
-            quantise_e(i)
-            if last:
-                project(0, 0, (0, 1, 2))
-                project(0, 1, (0, 1, 2))
-            attend(i)
-            if last:
-                project(1, 0, (0, 1, 2))
-            copy_reciprocal(i)
-            if not last:
-                regroup_v_second_half(i + 1)
-            divide_o(i)
-            quantise_w(i)
-            quantise_o(i)
-        for b, s in units[:3]:
-            project(b, s, (3,))
-        project(1, 1, (0, 1, 2, 3))
+        exponentials(0)
+        transpose_e(0)
+        transpose_k(1, 0)
+        scores(1)
+        quantise_v(0, 0)
+        quantise_v(0, 1)
+        reciprocal(0)
+        spread_reciprocal(0)
+        regroup_w(1, S)
+        regroup_v(V, 1, 0, 512)
+        regroup_v(V, 1, 512, 1024)
+        quantise_v(1, 0)
+        quantise_v(1, 1)
+        quantise_e(0)
+        negative_row_max(1)
+        attend(0)
+        copy_reciprocal(0)
+        divide_o(0)
+        quantise_w(1)
+        quantise_o(0)
+        exponentials(1)
+        transpose_q(1, S)
+        transpose_k(2, 0)
+        transpose_e(1)
+        scores(2)
+        reciprocal(1)
+        spread_reciprocal(1)
+        regroup_w(2, S)
+        regroup_v(V, 2, 0, 512)
+        regroup_v(V, 2, 512, 1024)
+        quantise_v(2, 0)
+        quantise_v(2, 1)
+        quantise_e(1)
+        negative_row_max(2)
+        attend(1)
+        copy_reciprocal(1)
+        divide_o(1)
+        quantise_w(2)
+        quantise_o(1)
+        exponentials(2)
+        transpose_k(3, 0)
+        transpose_e(2)
+        scores(3)
+        reciprocal(2)
+        spread_reciprocal(2)
+        regroup_w(3, S)
+        regroup_v(V, 3, 0, 512)
+        regroup_v(V, 3, 512, 768)
+        quantise_e(2)
+        negative_row_max(3)
+        attend(2)
+        copy_reciprocal(2)
+        divide_o(2)
+        quantise_w(3)
+        quantise_o(2)
+        exponentials(3)
+        transpose_e(3)
+        regroup_v(S, 3, 768, 1024)
+        quantise_v(3, 0)
+        reciprocal(3)
+        project(0, 0, (0, 2))
+        project(0, 1, (0, 2))
+        spread_reciprocal(3)
+        quantise_e(3)
+        quantise_v(3, 1)
+        attend(3)
+        project(0, 0, (1, 3))
+        project(0, 1, (1, 3))
         residual(0, 0)
+        copy_reciprocal(3)
+        divide_o(3)
         residual(0, 1)
-        residual(1, 0)
+        quantise_o(3)
+        project(1, 0, (0, 1, 2, 3))
         mean(0)
+        project(1, 1, (0, 2))
+        project(1, 1, (1, 3))
         variance(0)
+        centre_times_gamma(0)
+        residual(1, 0)
         residual(1, 1)
         mean(1)
         variance(1)
-        for b in range(B):
-            centre_times_gamma(b)
-        for b in range(B):
-            scale_shift_store(b)
+        scale_shift_store(0, 0)
+        centre_times_gamma(1)
+        scale_shift_store(0, 1)
+        scale_shift_store(1, 0)
+        scale_shift_store(1, 1)

@@ -45,6 +45,8 @@ def tile_crossattention_for_fusion_temporal_pb_kernel(tc, q, k, ki, v, vi, T, Wo
         make_identity(nc, ident_f[:])
         minus_half = const.tile([P, 1], F32, name="minus_half")
         nc.gpsimd.memset(minus_half[:], -0.5)
+        minus_one = const.tile([P, 1], F32, name="minus_one")
+        nc.gpsimd.memset(minus_one[:], -1.0)
 
         q_sb = [raw.tile([P, C], BF16, name="q_sb%d" % b) for b in range(B)]
         k_sb = [raw.tile([P, 4, C], BF16, name="k_sb%d" % i) for i in range(4)]
@@ -229,7 +231,7 @@ def tile_crossattention_for_fusion_temporal_pb_kernel(tc, q, k, ki, v, vi, T, Wo
 
         def reciprocal(i):
             recip[i] = small.tile([P, 1], F32, name="recip%d" % i)
-            nc.vector.reciprocal(out=recip[i][:], in_=row_sum[i][:])
+            nc.gpsimd.tensor_tensor(out=recip[i][:], in0=row_sum[i][:], in1=minus_one[:], op=ALU.pow)
 
         def spread_reciprocal(i):
             recip_ps[i] = psum.tile([P, P], F32, tag="bank", name="recip_ps%d" % i)
@@ -237,8 +239,8 @@ def tile_crossattention_for_fusion_temporal_pb_kernel(tc, q, k, ki, v, vi, T, Wo
                 out=recip_ps[i][:], lhsT=recip[i][:, 0:1].to_broadcast([P, P]), rhs=ident_f[:], start=True, stop=True
             )
 
-        def copy_reciprocal(i):
-            nc.vector.tensor_copy(out=recip_sb[i][:], in_=recip_ps[i][:])
+        def copy_reciprocal(i, copy=nc.vector.tensor_copy):
+            copy(out=recip_sb[i][:], in_=recip_ps[i][:])
 
         def regroup(copy, dst, src):
             copy(
@@ -259,11 +261,12 @@ def tile_crossattention_for_fusion_temporal_pb_kernel(tc, q, k, ki, v, vi, T, Wo
                 src = v_half_sb[n][:, :, lo - HALF * n : hi - HALF * n]
             regroup(copy, v_grouped[i][:, lo:hi, :], src)
 
-        def quantise_v(i, n):
+        def quantise_v(i, n=None):
+            cols = slice(0, DV) if n is None else half(n)
             nc.vector.quantize_mx(
-                out=v_codes[i][:, half(n)].bitcast(FP8X4),
-                scales=v_scales[i][:, half(n)],
-                in_=v_grouped[i][:, half(n), :].rearrange("p w j -> p (w j)"),
+                out=v_codes[i][:, cols].bitcast(FP8X4),
+                scales=v_scales[i][:, cols],
+                in_=v_grouped[i][:, cols, :].rearrange("p w j -> p (w j)"),
             )
 
         oT_ps = {}
@@ -415,18 +418,20 @@ def tile_crossattention_for_fusion_temporal_pb_kernel(tc, q, k, ki, v, vi, T, Wo
 
         y = {}
 
-        def scale_shift_store(b, n):
+        def scale_shift_store(b, n=None):
+            cols = slice(0, C) if n is None else half(n)
             if b not in y:
                 y[b] = work.tile([P, C], F32, tag="y", name="y%d" % b)
             nc.vector.scalar_tensor_tensor(
-                out=y[b][:, half(n)],
-                in0=centred[b][:, half(n)],
+                out=y[b][:, cols],
+                in0=centred[b][:, cols],
                 scalar=rstd[b][:],
-                in1=beta_sb[:, half(n)],
+                in1=beta_sb[:, cols],
                 op0=ALU.mult,
                 op1=ALU.add,
             )
-            nc.sync.dma_start(out=out[b, :, half(n)], in_=y[b][:, half(n)])
+            nc.sync.dma_start(out=out[b, :, cols], in_=y[b][:, cols])
+
 
         V = nc.vector.tensor_copy
         S = nc.scalar.copy
@@ -461,21 +466,20 @@ def tile_crossattention_for_fusion_temporal_pb_kernel(tc, q, k, ki, v, vi, T, Wo
         transpose_k_rows(0, 3, V)
         scores_by_rows(0)
         regroup_v(V, 0, 0, 512)
-        regroup_v(S, 0, 512, 1024)
+        regroup_v(S, 0, 768, 1024)
         negative_row_max(0)
+        regroup_v(V, 0, 512, 768)
         exponentials(0)
         transpose_e(0)
+        quantise_v(0)
         transpose_k(1, 0)
         scores(1)
-        quantise_v(0, 0)
-        quantise_v(0, 1)
         reciprocal(0)
         spread_reciprocal(0)
+        regroup_v(S, 1, 896, 1024)
         regroup_w(1, S)
-        regroup_v(V, 1, 0, 512)
-        regroup_v(V, 1, 512, 1024)
-        quantise_v(1, 0)
-        quantise_v(1, 1)
+        regroup_v(V, 1, 0, 896)
+        quantise_v(1)
         quantise_e(0)
         negative_row_max(1)
         attend(0)
@@ -490,11 +494,10 @@ def tile_crossattention_for_fusion_temporal_pb_kernel(tc, q, k, ki, v, vi, T, Wo
         scores(2)
         reciprocal(1)
         spread_reciprocal(1)
+        regroup_v(S, 2, 896, 1024)
         regroup_w(2, S)
-        regroup_v(V, 2, 0, 512)
-        regroup_v(V, 2, 512, 1024)
-        quantise_v(2, 0)
-        quantise_v(2, 1)
+        regroup_v(V, 2, 0, 896)
+        quantise_v(2)
         quantise_e(1)
         negative_row_max(2)
         attend(1)
@@ -509,8 +512,7 @@ def tile_crossattention_for_fusion_temporal_pb_kernel(tc, q, k, ki, v, vi, T, Wo
         reciprocal(2)
         spread_reciprocal(2)
         regroup_w(3, S)
-        regroup_v(V, 3, 0, 512)
-        regroup_v(V, 3, 512, 768)
+        regroup_v(V, 3, 0, 768)
         quantise_e(2)
         negative_row_max(3)
         attend(2)
@@ -520,9 +522,9 @@ def tile_crossattention_for_fusion_temporal_pb_kernel(tc, q, k, ki, v, vi, T, Wo
         quantise_o(2)
         exponentials(3)
         transpose_e(3)
+        reciprocal(3)
         regroup_v(S, 3, 768, 1024)
         quantise_v(3, 0)
-        reciprocal(3)
         project(0, 0, (0, 2))
         project(0, 1, (0, 2))
         spread_reciprocal(3)
@@ -532,7 +534,7 @@ def tile_crossattention_for_fusion_temporal_pb_kernel(tc, q, k, ki, v, vi, T, Wo
         project(0, 0, (1, 3))
         project(0, 1, (1, 3))
         residual(0, 0)
-        copy_reciprocal(3)
+        copy_reciprocal(3, S)
         divide_o(3)
         residual(0, 1)
         quantise_o(3)
@@ -546,8 +548,7 @@ def tile_crossattention_for_fusion_temporal_pb_kernel(tc, q, k, ki, v, vi, T, Wo
         residual(1, 1)
         mean(1)
         variance(1)
-        scale_shift_store(0, 0)
+        scale_shift_store(0)
         centre_times_gamma(1)
-        scale_shift_store(0, 1)
         scale_shift_store(1, 0)
         scale_shift_store(1, 1)

@@ -31,7 +31,7 @@ def tile_crossattention_for_fusion_temporal_pb_kernel(tc, q, k, ki, v, vi, T, Wo
         keep = ctx.enter_context(tc.tile_pool(name="keep", bufs=1))
         small = ctx.enter_context(tc.tile_pool(name="small", bufs=1))
         work = ctx.enter_context(tc.tile_pool(name="work", bufs=2))
-        psum = ctx.enter_context(tc.psum_pool(name="psum", bufs=8))
+        psum = ctx.enter_context(tc.psum_pool(name="psum", bufs=1))
         ctx.enter_context(tc.manual_schedule())
 
         units = [(b, s) for b in range(B) for s in range(2)]
@@ -95,14 +95,14 @@ def tile_crossattention_for_fusion_temporal_pb_kernel(tc, q, k, ki, v, vi, T, Wo
             nc.sync.dma_start(out=w_sb1[:], in_=Wout.rearrange("(g t p) n -> g p t n", g=2, t=4, p=P)[1])
 
         def warm_up(count):
-            scratch = psum.tile([P, P], F32, tag="bank", name="scratch")
+            scratch = psum.tile([P, P], F32, tag="s", bufs=1, name="scratch")
             for j in range(count):
                 nc.tensor.matmul(out=scratch[:], lhsT=ident_f[:], rhs=ident_f[:], start=True, stop=True)
 
         qT = [keep.tile([P, 4, P], F32, name="qT%d" % b) for b in range(B)]
 
         def transpose_q(b, copy=nc.scalar.copy):
-            bank = psum.tile([P, 4, P], F32, tag="bank", name="qT_ps%d" % b)
+            bank = psum.tile([P, 4, P], F32, tag="tr", bufs=1, name="qT_ps%d" % b)
             words = q_sb[b][:].bitcast(F32)
             for u in range(4):
                 nc.tensor.transpose(out=bank[:, u, :], in_=words[:, P * u : P * (u + 1)], identity=ident_f[:])
@@ -110,29 +110,32 @@ def tile_crossattention_for_fusion_temporal_pb_kernel(tc, q, k, ki, v, vi, T, Wo
 
         kT = {}
 
-        def transpose_k(i, vector_chunks):
-            banks = []
+        k_banks = {}
+
+        def k_to_psum(i):
+            k_banks[i] = []
             for u in range(4):
-                bank = psum.tile([P, 4, P], F32, tag="bank", name="kT_ps%d_%d" % (i, u))
+                bank = psum.tile([P, 4, P], F32, tag="kT", bufs=4, name="kT_ps%d_%d" % (i, u))
                 for a in range(4):
                     nc.tensor.transpose(
                         out=bank[:, a, :],
                         in_=k_sb[i][:, a, :].bitcast(F32)[:, P * u : P * (u + 1)],
                         identity=ident_f[:],
                     )
-                banks.append(bank)
+                k_banks[i].append(bank)
+
+        def k_from_psum(i):
             kT[i] = work.tile([P, 4, NK], F32, tag="kT", name="kT%d" % i)
             for u in range(4):
-                copy = nc.vector.tensor_copy if u >= 4 - vector_chunks else nc.scalar.copy
-                copy(
+                nc.scalar.copy(
                     out=kT[i][:, u, :].rearrange("p (n a) -> p n a", a=4),
-                    in_=banks[u][:].rearrange("p a n -> p n a"),
+                    in_=k_banks[i][u][:].rearrange("p a n -> p n a"),
                 )
 
         def transpose_k_rows(i, a, copy):
             if i not in kT:
                 kT[i] = work.tile([P, 4, NK], F32, tag="kT", name="kT%d" % i)
-            bank = psum.tile([P, 4, P], F32, tag="bank", name="kTr_ps%d_%d" % (i, a))
+            bank = psum.tile([P, 4, P], F32, tag="kT", bufs=4, name="kTr_ps%d_%d" % (i, a))
             words = k_sb[i][:, a, :].bitcast(F32)
             for u in range(4):
                 nc.tensor.transpose(out=bank[:, u, :], in_=words[:, P * u : P * (u + 1)], identity=ident_f[:])
@@ -142,7 +145,7 @@ def tile_crossattention_for_fusion_temporal_pb_kernel(tc, q, k, ki, v, vi, T, Wo
 
         def scores(i):
             b = units[i][0]
-            s_ps[i] = psum.tile([P, NK], F32, tag="bank", name="s_ps%d" % i)
+            s_ps[i] = psum.tile([P, NK], F32, tag="s", bufs=1, name="s_ps%d" % i)
             for u in range(4):
                 q_pairs = qT[b][:, u, :].bitcast(BF16).rearrange("p (m e) -> p e m", e=2)
                 k_pairs = kT[i][:, u, :].bitcast(BF16).rearrange("p (n e) -> p e n", e=2)
@@ -157,7 +160,7 @@ def tile_crossattention_for_fusion_temporal_pb_kernel(tc, q, k, ki, v, vi, T, Wo
 
         def scores_by_rows(i):
             b = units[i][0]
-            s_ps[i] = psum.tile([P, NK], F32, tag="bank", name="s_ps%d" % i)
+            s_ps[i] = psum.tile([P, NK], F32, tag="s", bufs=1, name="s_ps%d" % i)
             for a in range(4):
                 for u in range(4):
                     q_pairs = qT[b][:, u, :].bitcast(BF16).rearrange("p (m e) -> p e m", e=2)
@@ -204,7 +207,7 @@ def tile_crossattention_for_fusion_temporal_pb_kernel(tc, q, k, ki, v, vi, T, Wo
         e_grouped = {}
 
         def transpose_e(i):
-            bank = psum.tile([P, 2, P], F32, tag="bank", name="eT_ps%d" % i)
+            bank = psum.tile([P, 2, P], F32, tag="tr", bufs=1, name="eT_ps%d" % i)
             words = e_sb[i][:].bitcast(F32)
             for h in range(2):
                 nc.tensor.transpose(out=bank[:, h, :], in_=words[:, h : 2 * P : 2], identity=ident_f[:])
@@ -234,7 +237,7 @@ def tile_crossattention_for_fusion_temporal_pb_kernel(tc, q, k, ki, v, vi, T, Wo
             nc.gpsimd.tensor_tensor(out=recip[i][:], in0=row_sum[i][:], in1=minus_one[:], op=ALU.pow)
 
         def spread_reciprocal(i):
-            recip_ps[i] = psum.tile([P, P], F32, tag="bank", name="recip_ps%d" % i)
+            recip_ps[i] = psum.tile([P, P], F32, tag="tr", bufs=1, name="recip_ps%d" % i)
             nc.tensor.matmul(
                 out=recip_ps[i][:], lhsT=recip[i][:, 0:1].to_broadcast([P, P]), rhs=ident_f[:], start=True, stop=True
             )
@@ -271,9 +274,9 @@ def tile_crossattention_for_fusion_temporal_pb_kernel(tc, q, k, ki, v, vi, T, Wo
 
         oT_ps = {}
 
-        def attend(i):
-            for g in range(2):
-                oT_ps[i, g] = psum.tile([P, 4, P], F32, tag="bank", name="oT_ps%d_%d" % (i, g))
+        def attend(i, halves=(0, 1)):
+            for g in halves:
+                oT_ps[i, g] = psum.tile([P, 4, P], F32, tag="o", bufs=2, name="oT_ps%d_%d" % (i, g))
                 for t in range(4):
                     cols = slice(P * (4 * g + t), P * (4 * g + t + 1))
                     nc.tensor.matmul_mx(
@@ -287,7 +290,7 @@ def tile_crossattention_for_fusion_temporal_pb_kernel(tc, q, k, ki, v, vi, T, Wo
                     )
 
         def keep_warm(i, count):
-            scratch = psum.tile([P, HALF], F32, tag="bank", name="warm_ps%d" % i)
+            scratch = psum.tile([P, HALF], F32, tag="s", bufs=1, name="warm_ps%d" % i)
             for j in range(count):
                 nc.tensor.matmul_mx(
                     out=scratch[:],
@@ -303,9 +306,10 @@ def tile_crossattention_for_fusion_temporal_pb_kernel(tc, q, k, ki, v, vi, T, Wo
         o_codes = [keep.tile([P, 2 * P], U32, name="o_codes%d" % i, align_bytes=64) for i in range(4)]
         o_scales = [keep.tile([P, 2 * P], U8, name="o_scales%d" % i, align_bytes=64) for i in range(4)]
 
-        def divide_o(i):
-            o_grouped[i] = work.tile([P, 2, P, 4], BF16, tag="o_grouped", name="o_grouped%d" % i, align_bytes=64)
-            for g in range(2):
+        def divide_o(i, halves=(0, 1)):
+            if i not in o_grouped:
+                o_grouped[i] = work.tile([P, 2, P, 4], BF16, tag="o_grouped", name="o_grouped%d" % i, align_bytes=64)
+            for g in halves:
                 nc.vector.tensor_tensor(
                     out=o_grouped[i][:, g, :, :],
                     in0=oT_ps[i, g][:].rearrange("p t m -> p m t"),
@@ -349,7 +353,7 @@ def tile_crossattention_for_fusion_temporal_pb_kernel(tc, q, k, ki, v, vi, T, Wo
             for j in chunks:
                 g, n = divmod(j, 2)
                 if s == 0 and g == 0:
-                    x_ps[b, n] = psum.tile([P, HALF], F32, tag="bank", name="x_ps%d_%d" % (b, n))
+                    x_ps[b, n] = psum.tile([P, HALF], F32, tag="kT", bufs=4, name="x_ps%d_%d" % (b, n))
                 rows = slice(P * g, P * (g + 1))
                 nc.tensor.matmul_mx(
                     out=x_ps[b, n][:],
@@ -445,12 +449,12 @@ def tile_crossattention_for_fusion_temporal_pb_kernel(tc, q, k, ki, v, vi, T, Wo
         load_v_half(0, 1)
         load_k(1)
         load_v(1)
-        load_w_half(0, 1)
         load_q(1)
         load_k(2)
+        load_w_half(0, 1)
         load_v(2)
-        load_w(1)
         load_k(3)
+        load_w(1)
         load_v(3)
         load_t()
         load_gb()
@@ -461,85 +465,92 @@ def tile_crossattention_for_fusion_temporal_pb_kernel(tc, q, k, ki, v, vi, T, Wo
         transpose_q(0, S)
         transpose_k_rows(0, 0, S)
         transpose_k_rows(0, 1, V)
-        warm_up(2)
+        warm_up(4)
         transpose_k_rows(0, 2, S)
         transpose_k_rows(0, 3, V)
         scores_by_rows(0)
+        k_to_psum(1)
         regroup_v(V, 0, 0, 512)
         regroup_v(S, 0, 768, 1024)
         negative_row_max(0)
         regroup_v(V, 0, 512, 768)
         exponentials(0)
+        k_from_psum(1)
         transpose_e(0)
-        quantise_v(0)
-        transpose_k(1, 0)
         scores(1)
+        regroup_v(S, 1, 768, 1024)
+        transpose_q(1, S)
+        quantise_v(0, 0)
+        quantise_v(0, 1)
         reciprocal(0)
         spread_reciprocal(0)
-        regroup_v(S, 1, 896, 1024)
-        regroup_w(1, S)
-        regroup_v(V, 1, 0, 896)
-        quantise_v(1)
+        regroup_v(V, 1, 0, 768)
         quantise_e(0)
-        negative_row_max(1)
         attend(0)
+        k_to_psum(2)
+        negative_row_max(1)
+        quantise_v(1, 0)
+        quantise_v(1, 1)
         copy_reciprocal(0)
         divide_o(0)
-        quantise_w(1)
         quantise_o(0)
         exponentials(1)
-        transpose_q(1, S)
-        transpose_k(2, 0)
+        k_from_psum(2)
         transpose_e(1)
         scores(2)
+        k_to_psum(3)
         reciprocal(1)
         spread_reciprocal(1)
-        regroup_v(S, 2, 896, 1024)
-        regroup_w(2, S)
-        regroup_v(V, 2, 0, 896)
-        quantise_v(2)
+        regroup_w(1, S)
+        regroup_v(V, 2, 0, 1024)
         quantise_e(1)
-        negative_row_max(2)
         attend(1)
+        negative_row_max(2)
+        quantise_v(2, 0)
+        quantise_v(2, 1)
         copy_reciprocal(1)
         divide_o(1)
-        quantise_w(2)
+        quantise_w(1)
         quantise_o(1)
         exponentials(2)
-        transpose_k(3, 0)
+        k_from_psum(3)
         transpose_e(2)
         scores(3)
         reciprocal(2)
         spread_reciprocal(2)
-        regroup_w(3, S)
-        regroup_v(V, 3, 0, 768)
+        regroup_w(2, S)
+        regroup_w(3, V)
+        regroup_v(V, 3, 0, 512)
         quantise_e(2)
-        negative_row_max(3)
         attend(2)
+        negative_row_max(3)
         copy_reciprocal(2)
         divide_o(2)
+        quantise_w(2)
         quantise_w(3)
         quantise_o(2)
         exponentials(3)
         transpose_e(3)
         reciprocal(3)
-        regroup_v(S, 3, 768, 1024)
+        regroup_v(S, 3, 512, 1024)
         quantise_v(3, 0)
         project(0, 0, (0, 2))
         project(0, 1, (0, 2))
         spread_reciprocal(3)
         quantise_e(3)
+        residual(0, 0)
+        attend(3, (0,))
+        copy_reciprocal(3, S)
         quantise_v(3, 1)
-        attend(3)
         project(0, 0, (1, 3))
         project(0, 1, (1, 3))
-        residual(0, 0)
-        copy_reciprocal(3, S)
-        divide_o(3)
+        attend(3, (1,))
+        divide_o(3, (0,))
         residual(0, 1)
+        divide_o(3, (1,))
+        mean(0)
         quantise_o(3)
         project(1, 0, (0, 1, 2, 3))
-        mean(0)
         project(1, 1, (0, 2))
         project(1, 1, (1, 3))
         variance(0)

@@ -51,8 +51,7 @@ def tile_crossattention_for_fusion_temporal_pb_kernel(tc, q, k, ki, v, vi, T, Wo
         q_sb = [raw.tile([P, C], BF16, name="q_sb%d" % b) for b in range(B)]
         k_sb = [raw.tile([P, 4, C], BF16, name="k_sb%d" % i) for i in range(4)]
         v_sb = [raw.tile([P, 4, DV], BF16, name="v_sb%d" % i) for i in range(4)]
-        w_sb = [raw.tile([P, 4, HALF], BF16, name="w_sb%d" % j) for j in range(2)]
-        w_sb1 = raw.tile([P, 4, C], BF16, name="w_sb_last")
+        w_sb = [raw.tile([P, 4, HALF], BF16, name="w_sb%d" % j) for j in range(4)]
         v_half_sb = [raw.tile([P, 4, HALF], BF16, name="v_half_sb%d" % n) for n in range(2)]
         t_sb = raw.tile([P, B, C], BF16, name="t_sb")
         gamma_sb = const.tile([P, C], BF16, name="gamma_sb")
@@ -91,11 +90,8 @@ def tile_crossattention_for_fusion_temporal_pb_kernel(tc, q, k, ki, v, vi, T, Wo
             nc.sync.dma_start(out=gamma_sb[:], in_=gamma.partition_broadcast(P))
             nc.sync.dma_start(out=beta_sb[:], in_=beta.partition_broadcast(P))
 
-        def load_w(g):
-            nc.sync.dma_start(out=w_sb1[:], in_=Wout.rearrange("(g t p) n -> g p t n", g=2, t=4, p=P)[1])
-
         def warm_up(count):
-            scratch = psum.tile([P, P], F32, tag="s", bufs=1, name="scratch")
+            scratch = psum.tile([P, P], F32, tag="o", bufs=2, name="scratch")
             for j in range(count):
                 nc.tensor.matmul(out=scratch[:], lhsT=ident_f[:], rhs=ident_f[:], start=True, stop=True)
 
@@ -112,9 +108,11 @@ def tile_crossattention_for_fusion_temporal_pb_kernel(tc, q, k, ki, v, vi, T, Wo
 
         k_banks = {}
 
-        def k_to_psum(i):
+        def k_to_psum(i, warm=0):
             k_banks[i] = []
             for u in range(4):
+                if u == 1 and warm:
+                    warm_up(warm)
                 bank = psum.tile([P, 4, P], F32, tag="kT", bufs=4, name="kT_ps%d_%d" % (i, u))
                 for a in range(4):
                     nc.tensor.transpose(
@@ -227,23 +225,11 @@ def tile_crossattention_for_fusion_temporal_pb_kernel(tc, q, k, ki, v, vi, T, Wo
                 in_=e_grouped[i][:],
             )
 
-        recip_ps = {}
-        recip_sb = [keep.tile([P, P], F32, name="recip_sb%d" % i) for i in range(4)]
-
         recip = {}
 
         def reciprocal(i):
             recip[i] = small.tile([P, 1], F32, name="recip%d" % i)
             nc.gpsimd.tensor_tensor(out=recip[i][:], in0=row_sum[i][:], in1=minus_one[:], op=ALU.pow)
-
-        def spread_reciprocal(i):
-            recip_ps[i] = psum.tile([P, P], F32, tag="tr", bufs=1, name="recip_ps%d" % i)
-            nc.tensor.matmul(
-                out=recip_ps[i][:], lhsT=recip[i][:, 0:1].to_broadcast([P, P]), rhs=ident_f[:], start=True, stop=True
-            )
-
-        def copy_reciprocal(i, copy=nc.vector.tensor_copy):
-            copy(out=recip_sb[i][:], in_=recip_ps[i][:])
 
         def regroup(copy, dst, src):
             copy(
@@ -272,22 +258,53 @@ def tile_crossattention_for_fusion_temporal_pb_kernel(tc, q, k, ki, v, vi, T, Wo
                 in_=v_grouped[i][:, cols, :].rearrange("p w j -> p (w j)"),
             )
 
-        oT_ps = {}
+        o_ps = {}
+        o_sb = {}
+        o_grouped = {}
+        o_codes = [keep.tile([P, 2 * P], U32, name="o_codes%d" % i, align_bytes=64) for i in range(4)]
+        o_scales = [keep.tile([P, 2 * P], U8, name="o_scales%d" % i, align_bytes=64) for i in range(4)]
 
         def attend(i, halves=(0, 1)):
             for g in halves:
-                oT_ps[i, g] = psum.tile([P, 4, P], F32, tag="o", bufs=2, name="oT_ps%d_%d" % (i, g))
-                for t in range(4):
-                    cols = slice(P * (4 * g + t), P * (4 * g + t + 1))
-                    nc.tensor.matmul_mx(
-                        out=oT_ps[i, g][:, t, :],
-                        lhsT=v_codes[i][:, cols].bitcast(FP8X4),
-                        lhsT_scale=v_scales[i][:, cols],
-                        rhs=e_codes[i][:].bitcast(FP8X4),
-                        rhs_scale=e_scales[i][:],
-                        start=True,
-                        stop=True,
+                o_ps[i, g] = psum.tile([P, HALF], F32, tag="o", bufs=2, name="o_ps%d_%d" % (i, g))
+                nc.tensor.matmul_mx(
+                    out=o_ps[i, g][:],
+                    lhsT=e_codes[i][:].bitcast(FP8X4),
+                    lhsT_scale=e_scales[i][:],
+                    rhs=v_codes[i][:, half(g)].bitcast(FP8X4),
+                    rhs_scale=v_scales[i][:, half(g)],
+                    start=True,
+                    stop=True,
+                )
+
+        def divide_o(i, g, on_vector=False):
+            if i not in o_sb:
+                o_sb[i] = work.tile([P, 2, HALF], BF16, tag="o_sb", name="o_sb%d" % i)
+            if on_vector:
+                nc.vector.tensor_scalar(
+                    out=o_sb[i][:, g, :], in0=o_ps[i, g][:], scalar1=recip[i][:], scalar2=None, op0=ALU.mult
+                )
+            else:
+                nc.scalar.activation(out=o_sb[i][:, g, :], in_=o_ps[i, g][:], func=ACT.Copy, scale=recip[i][:])
+
+        o_banks = {}
+
+        def o_to_psum(i, halves=(0, 1)):
+            if i not in o_banks:
+                o_banks[i] = psum.tile([P, 4, P], F32, tag="tr", bufs=1, name="otr_ps%d" % i)
+                o_grouped[i] = work.tile([P, 2, 4 * P], BF16, tag="o_grouped", name="o_grouped%d" % i, align_bytes=64)
+            for g in halves:
+                words = o_sb[i][:, g, :].bitcast(F32)
+                for h in range(2):
+                    nc.tensor.transpose(
+                        out=o_banks[i][:, 2 * g + h, :], in_=words[:, h : 2 * P : 2], identity=ident_f[:]
                     )
+
+        def o_from_psum(i, copy):
+            copy(
+                out=o_grouped[i][:].bitcast(F32).rearrange("p g (m h) -> p g m h", h=2),
+                in_=o_banks[i][:].rearrange("p (g h) m -> p g m h", g=2),
+            )
 
         def keep_warm(i, count):
             scratch = psum.tile([P, HALF], F32, tag="s", bufs=1, name="warm_ps%d" % i)
@@ -302,26 +319,11 @@ def tile_crossattention_for_fusion_temporal_pb_kernel(tc, q, k, ki, v, vi, T, Wo
                     stop=True,
                 )
 
-        o_grouped = {}
-        o_codes = [keep.tile([P, 2 * P], U32, name="o_codes%d" % i, align_bytes=64) for i in range(4)]
-        o_scales = [keep.tile([P, 2 * P], U8, name="o_scales%d" % i, align_bytes=64) for i in range(4)]
-
-        def divide_o(i, halves=(0, 1)):
-            if i not in o_grouped:
-                o_grouped[i] = work.tile([P, 2, P, 4], BF16, tag="o_grouped", name="o_grouped%d" % i, align_bytes=64)
-            for g in halves:
-                nc.vector.tensor_tensor(
-                    out=o_grouped[i][:, g, :, :],
-                    in0=oT_ps[i, g][:].rearrange("p t m -> p m t"),
-                    in1=recip_sb[i][:].unsqueeze(2).to_broadcast([P, P, 4]),
-                    op=ALU.mult,
-                )
-
         def quantise_o(i):
             nc.vector.quantize_mx(
                 out=o_codes[i][:].bitcast(FP8X4),
                 scales=o_scales[i][:],
-                in_=o_grouped[i][:].rearrange("p g m t -> p (g m t)"),
+                in_=o_grouped[i][:].rearrange("p g n -> p (g n)"),
             )
 
         w_grouped = keep.tile([P, 2, C, 4], BF16, name="w_grouped", align_bytes=64)
@@ -330,13 +332,13 @@ def tile_crossattention_for_fusion_temporal_pb_kernel(tc, q, k, ki, v, vi, T, Wo
 
         def load_w_half(g, n):
             nc.sync.dma_start(
-                out=w_sb[n][:] if g == 0 else w_sb1[:, :, half(n)],
-                in_=Wout.rearrange("(g t p) n -> g p t n", g=2, t=4, p=P)[g][:, :, half(n)],
+                out=w_sb[2 * g + n][:],
+                in_=Wout.rearrange("(g p t) n -> g p t n", g=2, t=4, p=P)[g][:, :, half(n)],
             )
 
-        def regroup_w(j, copy=nc.scalar.copy):
+        def regroup_w(j, copy, lo=0, hi=HALF):
             g, n = divmod(j, 2)
-            regroup(copy, w_grouped[:, g, half(n), :], w_sb[n][:] if g == 0 else w_sb1[:, :, half(n)])
+            regroup(copy, w_grouped[:, g, HALF * n + lo : HALF * n + hi, :], w_sb[j][:, :, lo:hi])
 
         def quantise_w(j):
             g, n = divmod(j, 2)
@@ -436,7 +438,6 @@ def tile_crossattention_for_fusion_temporal_pb_kernel(tc, q, k, ki, v, vi, T, Wo
             )
             nc.sync.dma_start(out=out[b, :, cols], in_=y[b][:, cols])
 
-
         V = nc.vector.tensor_copy
         S = nc.scalar.copy
         load_w_half(0, 0)
@@ -449,12 +450,13 @@ def tile_crossattention_for_fusion_temporal_pb_kernel(tc, q, k, ki, v, vi, T, Wo
         load_v_half(0, 1)
         load_k(1)
         load_v(1)
+        load_w_half(0, 1)
         load_q(1)
         load_k(2)
-        load_w_half(0, 1)
         load_v(2)
         load_k(3)
-        load_w(1)
+        load_w_half(1, 0)
+        load_w_half(1, 1)
         load_v(3)
         load_t()
         load_gb()
@@ -465,96 +467,98 @@ def tile_crossattention_for_fusion_temporal_pb_kernel(tc, q, k, ki, v, vi, T, Wo
         transpose_q(0, S)
         transpose_k_rows(0, 0, S)
         transpose_k_rows(0, 1, V)
-        warm_up(4)
+        warm_up(2)
         transpose_k_rows(0, 2, S)
         transpose_k_rows(0, 3, V)
         scores_by_rows(0)
-        k_to_psum(1)
+        k_to_psum(1, 2)
         regroup_v(V, 0, 0, 512)
         regroup_v(S, 0, 768, 1024)
         negative_row_max(0)
         regroup_v(V, 0, 512, 768)
         exponentials(0)
+        reciprocal(0)
         k_from_psum(1)
         transpose_e(0)
         scores(1)
         regroup_v(S, 1, 768, 1024)
-        transpose_q(1, S)
         quantise_v(0, 0)
         quantise_v(0, 1)
-        reciprocal(0)
-        spread_reciprocal(0)
         regroup_v(V, 1, 0, 768)
         quantise_e(0)
+        transpose_q(1, S)
         attend(0)
         k_to_psum(2)
         negative_row_max(1)
-        quantise_v(1, 0)
-        quantise_v(1, 1)
-        copy_reciprocal(0)
-        divide_o(0)
-        quantise_o(0)
         exponentials(1)
+        reciprocal(1)
+        quantise_v(1)
+        regroup_w(1, V)
+        quantise_w(1)
         k_from_psum(2)
         transpose_e(1)
         scores(2)
+        regroup_v(S, 2, 768, 1024)
+        divide_o(0, 0, False)
+        divide_o(0, 1, False)
         k_to_psum(3)
-        reciprocal(1)
-        spread_reciprocal(1)
-        regroup_w(1, S)
-        regroup_v(V, 2, 0, 1024)
+        o_to_psum(0)
+        regroup_v(V, 2, 0, 768)
+        negative_row_max(2)
         quantise_e(1)
         attend(1)
-        negative_row_max(2)
-        quantise_v(2, 0)
-        quantise_v(2, 1)
-        copy_reciprocal(1)
-        divide_o(1)
-        quantise_w(1)
-        quantise_o(1)
         exponentials(2)
+        reciprocal(2)
+        o_from_psum(0, S)
+        quantise_v(2)
+        regroup_w(2, V)
         k_from_psum(3)
         transpose_e(2)
         scores(3)
-        reciprocal(2)
-        spread_reciprocal(2)
-        regroup_w(2, S)
-        regroup_w(3, V)
-        regroup_v(V, 3, 0, 512)
+        divide_o(1, 0, False)
+        divide_o(1, 1, False)
+        quantise_w(2)
+        quantise_o(0)
+        o_to_psum(1)
+        regroup_v(V, 3, 0, 768)
+        negative_row_max(3)
         quantise_e(2)
         attend(2)
-        negative_row_max(3)
-        copy_reciprocal(2)
-        divide_o(2)
-        quantise_w(2)
+        regroup_w(3, V)
         quantise_w(3)
-        quantise_o(2)
+        regroup_v(S, 3, 768, 1024)
         exponentials(3)
-        transpose_e(3)
         reciprocal(3)
-        regroup_v(S, 3, 512, 1024)
-        quantise_v(3, 0)
+        o_from_psum(1, S)
+        divide_o(2, 0, False)
+        transpose_e(3)
+        divide_o(2, 1, False)
+        quantise_o(1)
+        quantise_v(3)
         project(0, 0, (0, 2))
         project(0, 1, (0, 2))
-        spread_reciprocal(3)
         quantise_e(3)
-        residual(0, 0)
+        o_to_psum(2)
+        o_from_psum(2, S)
         attend(3, (0,))
-        copy_reciprocal(3, S)
-        quantise_v(3, 1)
+        residual(0, 0)
+        attend(3, (1,))
+        divide_o(3, 0, False)
+        divide_o(3, 1, False)
         project(0, 0, (1, 3))
         project(0, 1, (1, 3))
-        attend(3, (1,))
-        divide_o(3, (0,))
+        o_to_psum(3)
+        quantise_o(2)
         residual(0, 1)
-        divide_o(3, (1,))
         mean(0)
+        o_from_psum(3, S)
+        project(1, 0, (0, 2))
+        project(1, 0, (1, 3))
         quantise_o(3)
-        project(1, 0, (0, 1, 2, 3))
+        centre_times_gamma(0)
+        variance(0)
         project(1, 1, (0, 2))
         project(1, 1, (1, 3))
-        variance(0)
-        centre_times_gamma(0)
         residual(1, 0)
         residual(1, 1)
         mean(1)

@@ -20,7 +20,7 @@ HALF = 512
 SCALE = 1.0 / 32.0
 EPS = 1e-5
 FLOPS = 4 * (2 * P * NK * C + 2 * P * NK * DV + 2 * P * DV * C)
-V0_HALVES = True
+V0_HALVES = False
 
 
 def tile_crossattention_for_fusion_temporal_pb_kernel(tc, q, k, ki, v, vi, T, Wout, gamma, beta, out):
@@ -51,7 +51,8 @@ def tile_crossattention_for_fusion_temporal_pb_kernel(tc, q, k, ki, v, vi, T, Wo
         q_sb = [raw.tile([P, C], BF16, name="q_sb%d" % b) for b in range(B)]
         k_sb = [raw.tile([P, 4, C], BF16, name="k_sb%d" % i) for i in range(4)]
         v_sb = [raw.tile([P, 4, DV], BF16, name="v_sb%d" % i) for i in range(4)]
-        w_sb = [raw.tile([P, 4, HALF], BF16, name="w_sb%d" % j) for j in range(4)]
+        w_sb = [raw.tile([P, 4, HALF], BF16, name="w_sb%d" % j) for j in range(2)]
+        w_last = raw.tile([P, 4, C], BF16, name="w_last")
         v_half_sb = [raw.tile([P, 4, HALF], BF16, name="v_half_sb%d" % n) for n in range(2)]
         t_sb = raw.tile([P, B, C], BF16, name="t_sb")
         gamma_sb = const.tile([P, C], BF16, name="gamma_sb")
@@ -336,9 +337,12 @@ def tile_crossattention_for_fusion_temporal_pb_kernel(tc, q, k, ki, v, vi, T, Wo
                 in_=Wout.rearrange("(g p t) n -> g p t n", g=2, t=4, p=P)[g][:, :, half(n)],
             )
 
-        def regroup_w(j, copy, lo=0, hi=HALF):
+        def load_w_last():
+            nc.sync.dma_start(out=w_last[:], in_=Wout.rearrange("(g p t) n -> g p t n", g=2, t=4, p=P)[1])
+
+        def regroup_w(j, copy):
             g, n = divmod(j, 2)
-            regroup(copy, w_grouped[:, g, HALF * n + lo : HALF * n + hi, :], w_sb[j][:, :, lo:hi])
+            regroup(copy, w_grouped[:, g, half(n), :], w_sb[j][:] if g == 0 else w_last[:, :, half(n)])
 
         def quantise_w(j):
             g, n = divmod(j, 2)
@@ -446,8 +450,7 @@ def tile_crossattention_for_fusion_temporal_pb_kernel(tc, q, k, ki, v, vi, T, Wo
         load_k_rows(0, 1)
         load_k_rows(0, 2)
         load_k_rows(0, 3)
-        load_v_half(0, 0)
-        load_v_half(0, 1)
+        load_v(0)
         load_k(1)
         load_v(1)
         load_w_half(0, 1)
@@ -455,8 +458,7 @@ def tile_crossattention_for_fusion_temporal_pb_kernel(tc, q, k, ki, v, vi, T, Wo
         load_k(2)
         load_v(2)
         load_k(3)
-        load_w_half(1, 0)
-        load_w_half(1, 1)
+        load_w_last()
         load_v(3)
         load_t()
         load_gb()
@@ -472,18 +474,15 @@ def tile_crossattention_for_fusion_temporal_pb_kernel(tc, q, k, ki, v, vi, T, Wo
         transpose_k_rows(0, 3, V)
         scores_by_rows(0)
         k_to_psum(1, 2)
-        regroup_v(V, 0, 0, 512)
-        regroup_v(S, 0, 768, 1024)
         negative_row_max(0)
-        regroup_v(V, 0, 512, 768)
+        regroup_v(V, 0, 0, 1024)
         exponentials(0)
         reciprocal(0)
         k_from_psum(1)
         transpose_e(0)
         scores(1)
         regroup_v(S, 1, 768, 1024)
-        quantise_v(0, 0)
-        quantise_v(0, 1)
+        quantise_v(0)
         regroup_v(V, 1, 0, 768)
         quantise_e(0)
         transpose_q(1, S)

from contextlib import ExitStack

import concourse.mybir as mybir
from concourse.masks import make_identity

F32 = mybir.dt.float32
BF16 = mybir.dt.bfloat16
U32 = mybir.dt.uint32
U8 = mybir.dt.uint8
FP8X4 = mybir.dt.float8_e4m3fn_x4
ACT = mybir.ActivationFunctionType
ALU = mybir.AluOpType

P = 128
B = 2
NK = 512
C = 1024
DV = 1024
HALF = 512
SCALE = 1.0 / 32.0
EPS = 1e-5
FLOPS = 4 * (2 * P * NK * C + 2 * P * NK * DV + 2 * P * DV * C)
V0_HALVES = False


def tile_crossattention_for_fusion_temporal_pb_kernel(tc, q, k, ki, v, vi, T, Wout, gamma, beta, out):
    nc = tc.nc
    with ExitStack() as ctx:
        const = ctx.enter_context(tc.tile_pool(name="const", bufs=1))
        raw = ctx.enter_context(tc.tile_pool(name="raw", bufs=1))
        keep = ctx.enter_context(tc.tile_pool(name="keep", bufs=1))
        small = ctx.enter_context(tc.tile_pool(name="small", bufs=1))
        work = ctx.enter_context(tc.tile_pool(name="work", bufs=2))
        psum = ctx.enter_context(tc.psum_pool(name="psum", bufs=1))
        ctx.enter_context(tc.manual_schedule())

        units = [(b, s) for b in range(B) for s in range(2)]
        key_src = (k, ki)
        val_src = (v, vi)

        def half(n):
            return slice(HALF * n, HALF * (n + 1))

        ident_f = const.tile([P, P], F32, name="ident_f")
        make_identity(nc, ident_f[:])
        minus_half = const.tile([P, 1], F32, name="minus_half")
        nc.gpsimd.memset(minus_half[:], -0.5)
        minus_one = const.tile([P, 1], F32, name="minus_one")
        nc.gpsimd.memset(minus_one[:], -1.0)

        q_sb = [raw.tile([P, C], BF16, name="q_sb%d" % b) for b in range(B)]
        k_sb = [raw.tile([P, 4, C], BF16, name="k_sb%d" % i) for i in range(4)]
        v_sb = [raw.tile([P, 4, DV], BF16, name="v_sb%d" % i) for i in range(4)]
        w_sb = [raw.tile([P, 4, HALF], BF16, name="w_sb%d" % j) for j in range(2)]
        w_last = raw.tile([P, 4, C], BF16, name="w_last")
        v_half_sb = [raw.tile([P, 4, HALF], BF16, name="v_half_sb%d" % n) for n in range(2)]
        t_sb = raw.tile([P, B, C], BF16, name="t_sb")
        gamma_sb = const.tile([P, C], BF16, name="gamma_sb")
        beta_sb = const.tile([P, C], BF16, name="beta_sb")

        def load_q(b):
            nc.sync.dma_start(out=q_sb[b][:], in_=q[b, :, :])

        def load_k(i):
            b, s = units[i]
            nc.sync.dma_start(out=k_sb[i][:], in_=key_src[s][b, :, :].rearrange("(p a) c -> p a c", a=4))

        def load_k_rows(i, a):
            b, s = units[i]
            nc.sync.dma_start(out=k_sb[i][:, a, :], in_=key_src[s][b, P * a : P * (a + 1), :])

        def load_v_half(i, n):
            b, s = units[i]
            nc.sync.dma_start(
                out=v_half_sb[n][:],
                in_=val_src[s][b, :, half(n)].rearrange("(p j) w -> p j w", j=4),
            )

        def load_v(i):
            b, s = units[i]
            nc.sync.dma_start(out=v_sb[i][:], in_=val_src[s][b, :, :].rearrange("(p j) w -> p j w", j=4))

        def load_rest():
            load_t()
            load_gb()

        def load_t():
            nc.sync.dma_start(out=t_sb[:], in_=T.rearrange("b p c -> p b c"))

        def load_gb():
            nc.sync.dma_start(out=gamma_sb[:], in_=gamma.partition_broadcast(P))
            nc.sync.dma_start(out=beta_sb[:], in_=beta.partition_broadcast(P))

        def warm_up(count):
            scratch = psum.tile([P, P], F32, tag="o", bufs=2, name="scratch")
            for j in range(count):
                nc.tensor.matmul(out=scratch[:], lhsT=ident_f[:], rhs=ident_f[:], start=True, stop=True)

        qT = [keep.tile([P, 4, P], F32, name="qT%d" % b) for b in range(B)]

        def transpose_q(b, copy=nc.scalar.copy):
            bank = psum.tile([P, 4, P], F32, tag="tr", bufs=1, name="qT_ps%d" % b)
            words = q_sb[b][:].bitcast(F32)
            for u in range(4):
                nc.tensor.transpose(out=bank[:, u, :], in_=words[:, P * u : P * (u + 1)], identity=ident_f[:])
            copy(out=qT[b][:], in_=bank[:])

        kT = {}

        k_banks = {}

        def k_to_psum(i, warm=0):
            k_banks[i] = []
            for u in range(4):
                if u == 1 and warm:
                    warm_up(warm)
                bank = psum.tile([P, 4, P], F32, tag="kT", bufs=4, name="kT_ps%d_%d" % (i, u))
                for a in range(4):
                    nc.tensor.transpose(
                        out=bank[:, a, :],
                        in_=k_sb[i][:, a, :].bitcast(F32)[:, P * u : P * (u + 1)],
                        identity=ident_f[:],
                    )
                k_banks[i].append(bank)

        def k_from_psum(i):
            kT[i] = work.tile([P, 4, NK], F32, tag="kT", name="kT%d" % i)
            for u in range(4):
                nc.scalar.copy(
                    out=kT[i][:, u, :].rearrange("p (n a) -> p n a", a=4),
                    in_=k_banks[i][u][:].rearrange("p a n -> p n a"),
                )

        def transpose_k_rows(i, a, copy):
            if i not in kT:
                kT[i] = work.tile([P, 4, NK], F32, tag="kT", name="kT%d" % i)
            bank = psum.tile([P, 4, P], F32, tag="kT", bufs=4, name="kTr_ps%d_%d" % (i, a))
            words = k_sb[i][:, a, :].bitcast(F32)
            for u in range(4):
                nc.tensor.transpose(out=bank[:, u, :], in_=words[:, P * u : P * (u + 1)], identity=ident_f[:])
            copy(out=kT[i][:, a, :], in_=bank[:].rearrange("p u n -> p (u n)"))

        s_ps = {}

        def scores(i):
            b = units[i][0]
            s_ps[i] = psum.tile([P, NK], F32, tag="s", bufs=1, name="s_ps%d" % i)
            for u in range(4):
                q_pairs = qT[b][:, u, :].bitcast(BF16).rearrange("p (m e) -> p e m", e=2)
                k_pairs = kT[i][:, u, :].bitcast(BF16).rearrange("p (n e) -> p e n", e=2)
                for e in range(2):
                    nc.tensor.matmul(
                        out=s_ps[i][:],
                        lhsT=q_pairs[:, e, :],
                        rhs=k_pairs[:, e, :],
                        start=(u == 0 and e == 0),
                        stop=(u == 3 and e == 1),
                    )

        def scores_by_rows(i):
            b = units[i][0]
            s_ps[i] = psum.tile([P, NK], F32, tag="s", bufs=1, name="s_ps%d" % i)
            for a in range(4):
                for u in range(4):
                    q_pairs = qT[b][:, u, :].bitcast(BF16).rearrange("p (m e) -> p e m", e=2)
                    k_pairs = kT[i][:, a, P * u : P * (u + 1)].bitcast(BF16).rearrange("p (n e) -> p e n", e=2)
                    for e in range(2):
                        nc.tensor.matmul(
                            out=s_ps[i][:, P * a : P * (a + 1)],
                            lhsT=q_pairs[:, e, :],
                            rhs=k_pairs[:, e, :],
                            start=(u == 0 and e == 0),
                            stop=(u == 3 and e == 1),
                        )

        neg_max = {}

        def negative_row_max(i):
            scaled = work.tile([P, NK], BF16, tag="scaled", name="scaled%d" % i, bufs=1)
            neg_max[i] = small.tile([P, 1], F32, name="neg_max%d" % i)
            nc.vector.tensor_scalar(
                out=scaled[:],
                in0=s_ps[i][:],
                scalar1=-SCALE,
                scalar2=None,
                op0=ALU.mult,
                op1=ALU.min,
                accum_out=neg_max[i][:],
            )

        e_sb = {}
        row_sum = {}

        def exponentials(i):
            e_sb[i] = work.tile([P, NK], BF16, tag="e_sb", name="e_sb%d" % i)
            row_sum[i] = small.tile([P, 1], F32, name="row_sum%d" % i)
            nc.scalar.activation(
                out=e_sb[i][:],
                in_=s_ps[i][:],
                func=ACT.Exp,
                bias=neg_max[i][:],
                scale=SCALE,
                accum_out=row_sum[i][:],
            )

        e_grouped = {}

        def transpose_e(i):
            bank = psum.tile([P, 2, P], F32, tag="tr", bufs=1, name="eT_ps%d" % i)
            words = e_sb[i][:].bitcast(F32)
            for h in range(2):
                nc.tensor.transpose(out=bank[:, h, :], in_=words[:, h : 2 * P : 2], identity=ident_f[:])
            e_grouped[i] = work.tile([P, P * 4], BF16, tag="e_grouped", name="e_grouped%d" % i, align_bytes=64)
            nc.scalar.copy(
                out=e_grouped[i][:].bitcast(F32).rearrange("p (m h) -> p m h", h=2),
                in_=bank[:].rearrange("p h m -> p m h"),
            )

        e_codes = [keep.tile([P, P], U32, name="e_codes%d" % i, align_bytes=64) for i in range(4)]
        e_scales = [keep.tile([P, P], U8, name="e_scales%d" % i, align_bytes=64) for i in range(4)]

        def quantise_e(i):
            nc.vector.quantize_mx(
                out=e_codes[i][:].bitcast(FP8X4),
                scales=e_scales[i][:],
                in_=e_grouped[i][:],
            )

        recip = {}

        def reciprocal(i):
            recip[i] = small.tile([P, 1], F32, name="recip%d" % i)
            nc.gpsimd.tensor_tensor(out=recip[i][:], in0=row_sum[i][:], in1=minus_one[:], op=ALU.pow)

        def regroup(copy, dst, src):
            copy(
                out=dst.rearrange("p (c i) t -> p c t i", i=4),
                in_=src.rearrange("p t (c i) -> p c t i", i=4),
            )

        v_grouped = {}
        v_codes = [keep.tile([P, DV], U32, name="v_codes%d" % i, align_bytes=64) for i in range(4)]
        v_scales = [keep.tile([P, DV], U8, name="v_scales%d" % i, align_bytes=64) for i in range(4)]

        def regroup_v(copy, i, lo, hi):
            if i not in v_grouped:
                v_grouped[i] = work.tile([P, DV, 4], BF16, tag="v_grouped", name="v_grouped%d" % i, align_bytes=64)
            src = v_sb[i][:, :, lo:hi]
            if i == 0 and V0_HALVES:
                n = lo // HALF
                src = v_half_sb[n][:, :, lo - HALF * n : hi - HALF * n]
            regroup(copy, v_grouped[i][:, lo:hi, :], src)

        def quantise_v(i, n=None):
            cols = slice(0, DV) if n is None else half(n)
            nc.vector.quantize_mx(
                out=v_codes[i][:, cols].bitcast(FP8X4),
                scales=v_scales[i][:, cols],
                in_=v_grouped[i][:, cols, :].rearrange("p w j -> p (w j)"),
            )

        o_ps = {}
        o_sb = {}
        o_grouped = {}
        o_codes = [keep.tile([P, 2 * P], U32, name="o_codes%d" % i, align_bytes=64) for i in range(4)]
        o_scales = [keep.tile([P, 2 * P], U8, name="o_scales%d" % i, align_bytes=64) for i in range(4)]

        def attend(i, halves=(0, 1)):
            for g in halves:
                o_ps[i, g] = psum.tile([P, HALF], F32, tag="o", bufs=2, name="o_ps%d_%d" % (i, g))
                nc.tensor.matmul_mx(
                    out=o_ps[i, g][:],
                    lhsT=e_codes[i][:].bitcast(FP8X4),
                    lhsT_scale=e_scales[i][:],
                    rhs=v_codes[i][:, half(g)].bitcast(FP8X4),
                    rhs_scale=v_scales[i][:, half(g)],
                    start=True,
                    stop=True,
                )

        def divide_o(i, g, on_vector=False):
            if i not in o_sb:
                o_sb[i] = work.tile([P, 2, HALF], BF16, tag="o_sb", name="o_sb%d" % i)
            if on_vector:
                nc.vector.tensor_scalar(
                    out=o_sb[i][:, g, :], in0=o_ps[i, g][:], scalar1=recip[i][:], scalar2=None, op0=ALU.mult
                )
            else:
                nc.scalar.activation(out=o_sb[i][:, g, :], in_=o_ps[i, g][:], func=ACT.Copy, scale=recip[i][:])

        o_banks = {}

        def o_to_psum(i, halves=(0, 1)):
            if i not in o_banks:
                o_banks[i] = psum.tile([P, 4, P], F32, tag="tr", bufs=1, name="otr_ps%d" % i)
                o_grouped[i] = work.tile([P, 2, 4 * P], BF16, tag="o_grouped", name="o_grouped%d" % i, align_bytes=64)
            for g in halves:
                words = o_sb[i][:, g, :].bitcast(F32)
                for h in range(2):
                    nc.tensor.transpose(
                        out=o_banks[i][:, 2 * g + h, :], in_=words[:, h : 2 * P : 2], identity=ident_f[:]
                    )

        def o_from_psum(i, copy):
            copy(
                out=o_grouped[i][:].bitcast(F32).rearrange("p g (m h) -> p g m h", h=2),
                in_=o_banks[i][:].rearrange("p (g h) m -> p g m h", g=2),
            )

        def keep_warm(i, count):
            scratch = psum.tile([P, HALF], F32, tag="s", bufs=1, name="warm_ps%d" % i)
            for j in range(count):
                nc.tensor.matmul_mx(
                    out=scratch[:],
                    lhsT=e_codes[i][:].bitcast(FP8X4),
                    lhsT_scale=e_scales[i][:],
                    rhs=v_codes[i][:, half(j % 2)].bitcast(FP8X4),
                    rhs_scale=v_scales[i][:, half(j % 2)],
                    start=True,
                    stop=True,
                )

        def quantise_o(i):
            nc.vector.quantize_mx(
                out=o_codes[i][:].bitcast(FP8X4),
                scales=o_scales[i][:],
                in_=o_grouped[i][:].rearrange("p g n -> p (g n)"),
            )

        w_grouped = keep.tile([P, 2, C, 4], BF16, name="w_grouped", align_bytes=64)
        w_codes = keep.tile([P, 2, C], U32, name="w_codes", align_bytes=64)
        w_scales = keep.tile([P, 2, C], U8, name="w_scales", align_bytes=64)

        def load_w_half(g, n):
            nc.sync.dma_start(
                out=w_sb[2 * g + n][:],
                in_=Wout.rearrange("(g p t) n -> g p t n", g=2, t=4, p=P)[g][:, :, half(n)],
            )

        def load_w_last():
            nc.sync.dma_start(out=w_last[:], in_=Wout.rearrange("(g p t) n -> g p t n", g=2, t=4, p=P)[1])

        def regroup_w(j, copy):
            g, n = divmod(j, 2)
            regroup(copy, w_grouped[:, g, half(n), :], w_sb[j][:] if g == 0 else w_last[:, :, half(n)])

        def quantise_w(j):
            g, n = divmod(j, 2)
            nc.vector.quantize_mx(
                out=w_codes[:, g, half(n)].bitcast(FP8X4),
                scales=w_scales[:, g, half(n)],
                in_=w_grouped[:, g, half(n), :].rearrange("p w j -> p (w j)"),
            )

        x_ps = {}

        def project(b, s, chunks):
            i = 2 * b + s
            for j in chunks:
                g, n = divmod(j, 2)
                if s == 0 and g == 0:
                    x_ps[b, n] = psum.tile([P, HALF], F32, tag="kT", bufs=4, name="x_ps%d_%d" % (b, n))
                rows = slice(P * g, P * (g + 1))
                nc.tensor.matmul_mx(
                    out=x_ps[b, n][:],
                    lhsT=o_codes[i][:, rows].bitcast(FP8X4),
                    lhsT_scale=o_scales[i][:, rows],
                    rhs=w_codes[:, g, half(n)].bitcast(FP8X4),
                    rhs_scale=w_scales[:, g, half(n)],
                    start=(s == 0 and g == 0),
                    stop=(s == 1 and g == 1),
                )

        hidden = {}
        half_sums = {}
        neg_mean = {}
        centred = {}
        rstd = {}

        def residual(b, n):
            if n == 0:
                hidden[b] = work.tile([P, C], F32, tag="hidden", name="hidden%d" % b)
                half_sums[b] = small.tile([P, 2], F32, name="half_sums%d" % b)
            nc.vector.scalar_tensor_tensor(
                out=hidden[b][:, half(n)],
                in0=x_ps[b, n][:],
                scalar=1.0,
                in1=t_sb[:, b, half(n)],
                op0=ALU.mult,
                op1=ALU.add,
                accum_out=half_sums[b][:, n : n + 1],
            )

        def mean(b):
            neg_mean[b] = small.tile([P, 1], F32, name="neg_mean%d" % b)
            nc.vector.tensor_scalar(
                out=neg_mean[b][:],
                in0=half_sums[b][:, 0:1],
                scalar1=half_sums[b][:, 1:2],
                scalar2=-1.0 / C,
                op0=ALU.add,
                op1=ALU.mult,
            )

        def variance(b):
            squares = work.tile([P, C], BF16, tag="squares", name="squares%d" % b, bufs=1)
            square_sum = small.tile([P, 1], F32, name="square_sum%d" % b)
            nc.scalar.activation(
                out=squares[:],
                in_=hidden[b][:],
                func=ACT.Square,
                bias=neg_mean[b][:],
                scale=1.0,
                accum_out=square_sum[:],
            )
            var_eps = small.tile([P, 1], F32, name="var_eps%d" % b)
            nc.gpsimd.tensor_scalar(
                out=var_eps[:], in0=square_sum[:], scalar1=1.0 / C, scalar2=EPS, op0=ALU.mult, op1=ALU.add
            )
            rstd[b] = small.tile([P, 1], F32, name="rstd%d" % b)
            nc.gpsimd.tensor_tensor(out=rstd[b][:], in0=var_eps[:], in1=minus_half[:], op=ALU.pow)

        def centre_times_gamma(b):
            centred[b] = work.tile([P, C], F32, tag="centred", name="centred%d" % b)
            nc.vector.scalar_tensor_tensor(
                out=centred[b][:], in0=hidden[b][:], scalar=neg_mean[b][:], in1=gamma_sb[:], op0=ALU.add, op1=ALU.mult
            )

        y = {}

        def scale_shift_store(b, n=None):
            cols = slice(0, C) if n is None else half(n)
            if b not in y:
                y[b] = work.tile([P, C], F32, tag="y", name="y%d" % b)
            nc.vector.scalar_tensor_tensor(
                out=y[b][:, cols],
                in0=centred[b][:, cols],
                scalar=rstd[b][:],
                in1=beta_sb[:, cols],
                op0=ALU.mult,
                op1=ALU.add,
            )
            nc.sync.dma_start(out=out[b, :, cols], in_=y[b][:, cols])

        V = nc.vector.tensor_copy
        S = nc.scalar.copy
        load_w_half(0, 0)
        load_q(0)
        load_k_rows(0, 0)
        load_k_rows(0, 1)
        load_k_rows(0, 2)
        load_k_rows(0, 3)
        load_v(0)
        load_k(1)
        load_v(1)
        load_w_half(0, 1)
        load_q(1)
        load_k(2)
        load_v(2)
        load_k(3)
        load_w_last()
        load_v(3)
        load_t()
        load_gb()
        warm_up(6)
        warm_up(2)
        regroup_w(0, V)
        quantise_w(0)
        transpose_q(0, S)
        transpose_k_rows(0, 0, S)
        transpose_k_rows(0, 1, V)
        warm_up(2)
        transpose_k_rows(0, 2, S)
        transpose_k_rows(0, 3, V)
        scores_by_rows(0)
        k_to_psum(1, 2)
        negative_row_max(0)
        regroup_v(V, 0, 0, 1024)
        exponentials(0)
        reciprocal(0)
        k_from_psum(1)
        transpose_e(0)
        scores(1)
        regroup_v(S, 1, 768, 1024)
        quantise_v(0)
        regroup_v(V, 1, 0, 768)
        quantise_e(0)
        transpose_q(1, S)
        attend(0)
        k_to_psum(2)
        negative_row_max(1)
        exponentials(1)
        reciprocal(1)
        quantise_v(1)
        regroup_w(1, V)
        quantise_w(1)
        k_from_psum(2)
        transpose_e(1)
        scores(2)
        regroup_v(S, 2, 768, 1024)
        divide_o(0, 0, False)
        divide_o(0, 1, False)
        k_to_psum(3)
        o_to_psum(0)
        regroup_v(V, 2, 0, 768)
        negative_row_max(2)
        quantise_e(1)
        attend(1)
        exponentials(2)
        reciprocal(2)
        o_from_psum(0, S)
        quantise_v(2)
        regroup_w(2, V)
        k_from_psum(3)
        transpose_e(2)
        scores(3)
        divide_o(1, 0, False)
        divide_o(1, 1, False)
        quantise_w(2)
        quantise_o(0)
        o_to_psum(1)
        regroup_v(V, 3, 0, 768)
        negative_row_max(3)
        quantise_e(2)
        attend(2)
        regroup_w(3, V)
        quantise_w(3)
        regroup_v(S, 3, 768, 1024)
        exponentials(3)
        reciprocal(3)
        o_from_psum(1, S)
        divide_o(2, 0, False)
        transpose_e(3)
        divide_o(2, 1, False)
        quantise_o(1)
        quantise_v(3)
        project(0, 0, (0, 2))
        project(0, 1, (0, 2))
        quantise_e(3)
        o_to_psum(2)
        o_from_psum(2, S)
        attend(3, (0,))
        residual(0, 0)
        attend(3, (1,))
        divide_o(3, 0, False)
        divide_o(3, 1, False)
        project(0, 0, (1, 3))
        project(0, 1, (1, 3))
        o_to_psum(3)
        quantise_o(2)
        residual(0, 1)
        mean(0)
        o_from_psum(3, S)
        project(1, 0, (0, 2))
        project(1, 0, (1, 3))
        quantise_o(3)
        centre_times_gamma(0)
        variance(0)
        project(1, 1, (0, 2))
        project(1, 1, (1, 3))
        residual(1, 0)
        residual(1, 1)
        mean(1)
        variance(1)
        scale_shift_store(0)
        centre_times_gamma(1)
        scale_shift_store(1, 0)
        scale_shift_store(1, 1)
